import numpy as np
import ml_dtypes


def mxq(x, axis, fmt="e4m3"):
    dtype, down = {"e4m3": (ml_dtypes.float8_e4m3fn, 7), "e5m2": (ml_dtypes.float8_e5m2, 14)}[fmt]
    v = np.moveaxis(np.asarray(x, np.float32).astype(ml_dtypes.bfloat16).astype(np.float64), axis, -1)
    blocks = v.reshape(v.shape[:-1] + (-1, 32))
    amax = np.abs(blocks).max(-1, keepdims=True)
    byte = np.maximum(np.where(amax > 0, np.frexp(amax)[1] - 1 + 127, 0) - down, 1)
    scale = np.exp2(byte - 127.0)
    codes = (blocks / scale).astype(np.float32).astype(dtype).astype(np.float64)
    return np.moveaxis((codes * scale).reshape(v.shape), -1, axis)


WIDE = False


def mx_kscale(k):
    if not WIDE:
        return np.ones(k)
    levels = np.array([10, -10, 5, -5, 0])
    a = np.random.permutation(np.resize(levels, k // 512 * 4)).reshape(k // 512, 4)
    idx = np.arange(k)
    return np.exp2(a[idx // 512, idx % 128 // 32])


BF16 = ml_dtypes.bfloat16


def bf(x):
    return np.asarray(x, np.float32).astype(BF16)


def f64(x):
    return np.asarray(x).astype(np.float64)


N, F_IN, F_OUT, H, SD = 2048, 512, 512, 8, 3
SLOPE = 0.2
NEG = -1e9


def leaky_relu(t):
    return np.where(t >= 0.0, t, SLOPE * t)


def elu(t):
    return np.where(t > 0.0, t, np.exp(np.minimum(t, 0.0)) - 1.0)


def setup_inputs():
    s = mx_kscale(F_IN)
    return {
        "node_features": bf(np.random.standard_normal((N, F_IN)) * 1.5 * s),
        "q": bf(np.random.standard_normal((N, H)) * 1.875),
        "k": bf(np.random.standard_normal((N, H)) * 1.875),
        "edges_features_distance": bf(np.random.uniform(size=(N, N)) * 0.0625),
        "edges_features_bond": bf(np.random.uniform(size=(N, N))),
        "degree_matrix": bf(np.random.randint(0, 2, (N, N))),
        "Wv": bf(np.random.standard_normal((F_IN, F_OUT)) * 4.5 / s[:, None]),
        "w_bond": bf(1.5 + 0.1 * np.random.standard_normal(1)),
        "w_bond_contrib": bf(1.25 + 0.1 * np.random.standard_normal(1)),
        "w_gauss": bf(-32.0 + 2.0 * np.random.standard_normal(1)),
    }


def reference(node_features, q, k, edges_features_distance, edges_features_bond, degree_matrix, Wv, w_bond, w_bond_contrib, w_gauss):
    v = (mxq(f64(node_features), 1, "e4m3") @ mxq(f64(Wv), 0, "e4m3")) * (1.0 / np.sqrt(F_IN))
    qk = (f64(q) + f64(k)) / np.sqrt(H)
    bond = f64(edges_features_bond) * (f64(w_bond)[0] * f64(w_bond_contrib)[0])
    gauss = f64(edges_features_distance) * f64(w_gauss)[0]
    edge = bond + gauss
    mask = np.where(f64(degree_matrix) > 0.0, 0.0, NEG)
    attn_sum = np.zeros((N, N))
    for h in range(H):
        scores = leaky_relu(qk[:, h][:, None] + edge) + mask
        e = np.exp(scores - scores.max(axis=0, keepdims=True))
        attn_sum = attn_sum + e / e.sum(axis=0, keepdims=True)
    attn_mean = attn_sum / H
    aggregated = mxq(attn_mean, 1, "e4m3") @ mxq(v, 0, "e4m3")
    return elu(aggregated)

@@ -1,0 +1,375 @@
+import math
+from contextlib import ExitStack
+
+import concourse.mybir as mybir
+from concourse.masks import make_identity
+
+F32 = mybir.dt.float32
+BF16 = mybir.dt.bfloat16
+U32 = mybir.dt.uint32
+U8 = mybir.dt.uint8
+FP8X4 = mybir.dt.float8_e4m3fn_x4
+ALU = mybir.AluOpType
+ACT = mybir.ActivationFunctionType
+AX = mybir.AxisListType
+
+P = 128
+PACK = 4
+K_PASS = P * PACK
+BANK = 512
+
+N = 2048
+F_IN = 512
+F_OUT = 512
+H = 8
+SLOPE = 0.2
+RISE = 1.0 - SLOPE
+NO_EDGE = -1.0e9
+
+ROW_TILES = N // P
+CB = BANK // P
+CHUNKS = ROW_TILES // CB
+PASSES = N // K_PASS
+JT = 2
+PANEL = JT * P
+PANELS = N // PANEL
+
+FLOPS = 2 * N * F_IN * F_OUT + 2 * N * N * F_OUT
+
+
+def tile_egatlayer_pa_kernel(
+    tc,
+    node_features,
+    q,
+    k,
+    edges_features_distance,
+    edges_features_bond,
+    degree_matrix,
+    Wv,
+    w_bond,
+    w_bond_contrib,
+    w_gauss,
+    out,
+):
+    nc = tc.nc
+    bond_rows = edges_features_bond.rearrange("(p it) j -> p it j", it=ROW_TILES)
+    dist_rows = edges_features_distance.rearrange("(p it) j -> p it j", it=ROW_TILES)
+    degree_rows = degree_matrix.rearrange("(p it) j -> p it j", it=ROW_TILES)
+    out_rows = out.rearrange("(p it) f -> p it f", it=ROW_TILES)
+
+    with ExitStack() as ctx:
+        const = ctx.enter_context(tc.tile_pool(name="const", bufs=1))
+        keep = ctx.enter_context(tc.tile_pool(name="keep", bufs=1))
+        edge = ctx.enter_context(tc.tile_pool(name="edge", bufs=6))
+        stage = ctx.enter_context(tc.tile_pool(name="stage", bufs=2))
+        small = ctx.enter_context(tc.tile_pool(name="small", bufs=3))
+        psum = ctx.enter_context(tc.psum_pool(name="psum", bufs=8))
+
+        ident_f = const.tile([P, P], F32)
+        make_identity(nc, ident_f[:])
+        ident_b = const.tile([P, P], BF16)
+        make_identity(nc, ident_b[:])
+
+        w_bond_sb = const.tile([P, 1], BF16)
+        nc.sync.dma_start(out=w_bond_sb[:], in_=w_bond.partition_broadcast(P))
+        w_contrib_sb = const.tile([P, 1], BF16)
+        nc.sync.dma_start(out=w_contrib_sb[:], in_=w_bond_contrib.partition_broadcast(P))
+        w_gauss_sb = const.tile([P, 1], BF16)
+        nc.sync.dma_start(out=w_gauss_sb[:], in_=w_gauss.partition_broadcast(P))
+        bond_weight = const.tile([P, 1], F32)
+        nc.vector.tensor_tensor(out=bond_weight[:], in0=w_bond_sb[:], in1=w_contrib_sb[:], op=ALU.mult)
+        gauss_weight = const.tile([P, 1], F32)
+        nc.vector.tensor_copy(out=gauss_weight[:], in_=w_gauss_sb[:])
+
+        q_sb = const.tile([P, ROW_TILES * H], BF16)
+        nc.sync.dma_start(out=q_sb[:], in_=q.rearrange("(p it) h -> p (it h)", it=ROW_TILES))
+        k_sb = const.tile([P, ROW_TILES * H], BF16)
+        nc.sync.dma_start(out=k_sb[:], in_=k.rearrange("(p it) h -> p (it h)", it=ROW_TILES))
+        q_plus_k = const.tile([P, ROW_TILES * H], F32)
+        nc.vector.tensor_tensor(out=q_plus_k[:], in0=q_sb[:], in1=k_sb[:], op=ALU.add)
+        a_sb = const.tile([P, ROW_TILES * H], F32)
+        nc.vector.tensor_scalar_mul(out=a_sb[:], in0=q_plus_k[:], scalar1=1.0 / math.sqrt(H))
+        neg_a = const.tile([P, ROW_TILES * H], F32)
+        nc.vector.tensor_scalar_mul(out=neg_a[:], in0=q_plus_k[:], scalar1=-1.0 / math.sqrt(H))
+        a_over_rise = const.tile([P, ROW_TILES * H], F32)
+        nc.vector.tensor_scalar_mul(out=a_over_rise[:], in0=q_plus_k[:], scalar1=1.0 / (RISE * math.sqrt(H)))
+
+        a_t_ps = psum.tile([P, BANK], F32, tag="bank")
+        nc.tensor.transpose(out=a_t_ps[:, :P], in_=a_sb[:], identity=ident_f[:])
+        a_tile_top = const.tile([P, 1], F32)
+        nc.vector.tensor_reduce(out=a_tile_top[:], in_=a_t_ps[:, :P], axis=AX.X, op=ALU.max)
+        a_spread_ps = psum.tile([P, BANK], F32, tag="bank")
+        nc.tensor.matmul(
+            out=a_spread_ps[:, :P],
+            lhsT=a_tile_top[:, 0:1].to_broadcast([P, P]),
+            rhs=ident_f[:],
+            start=True,
+            stop=True,
+        )
+        a_top = const.tile([P, H], F32)
+        nc.vector.tensor_reduce(
+            out=a_top[:],
+            in_=a_spread_ps[:, :P].rearrange("p (it h) -> p h it", h=H),
+            axis=AX.X,
+            op=ALU.max,
+        )
+
+        v_codes = keep.tile([P, PASSES, F_OUT], U32, align_bytes=64)
+        v_scales = keep.tile([P, PASSES, F_OUT], U8, align_bytes=64)
+        attn_codes = keep.tile([P, PASSES, N], U32, align_bytes=64)
+        attn_scales = keep.tile([P, PASSES, N], U8, align_bytes=64)
+
+        def prepare_edges(panel, chunk):
+            rows = slice(chunk * CB, (chunk + 1) * CB)
+            cols = slice(panel * PANEL, (panel + 1) * PANEL)
+            bond_t = stage.tile([P, CB * PANEL], BF16, tag="bond")
+            dist_t = stage.tile([P, CB * PANEL], BF16, tag="dist")
+            degree_t = stage.tile([P, CB * PANEL], BF16, tag="degree")
+            for sb, rows_view in ((bond_t, bond_rows), (dist_t, dist_rows), (degree_t, degree_rows)):
+                nc.sync.dma_start(
+                    out=sb[:].rearrange("p (b j) -> p b j", b=CB), in_=rows_view[:, rows, cols]
+                )
+            gauss_t = stage.tile([P, CB * PANEL], F32, tag="gauss")
+            nc.scalar.activation(out=gauss_t[:], in_=dist_t[:], func=ACT.Copy, scale=gauss_weight[:, 0:1])
+            mask_t = stage.tile([P, CB * PANEL], BF16, tag="mask")
+            nc.vector.tensor_scalar(
+                out=mask_t[:], in0=degree_t[:], scalar1=0.0, scalar2=NO_EDGE / RISE, op0=ALU.is_le, op1=ALU.mult
+            )
+            e_t = edge.tile([P, CB * PANEL], F32, tag="e")
+            nc.vector.scalar_tensor_tensor(
+                out=e_t[:], in0=bond_t[:], scalar=bond_weight[:, 0:1], in1=gauss_t[:], op0=ALU.mult, op1=ALU.add
+            )
+            shared_t = edge.tile([P, CB * PANEL], F32, tag="shared")
+            nc.vector.scalar_tensor_tensor(
+                out=shared_t[:], in0=e_t[:], scalar=SLOPE / RISE, in1=mask_t[:], op0=ALU.mult, op1=ALU.add
+            )
+            return e_t, shared_t
+
+        def block(tile_ap, b, jt):
+            start = b * PANEL + jt * P
+            return tile_ap[:, start : start + P]
+
+        def softmax_shifts(shared_tiles):
+            shared_top = small.tile([P, JT, CHUNKS], F32, tag="shared_top")
+            for chunk in range(CHUNKS):
+                for jt in range(JT):
+                    bank = psum.tile([P, BANK], F32, tag="bank")
+                    for b in range(CB):
+                        nc.tensor.transpose(
+                            out=bank[:, b * P : (b + 1) * P],
+                            in_=block(shared_tiles[chunk], b, jt),
+                            identity=ident_f[:],
+                        )
+                    nc.vector.tensor_reduce(
+                        out=shared_top[:, jt, chunk : chunk + 1], in_=bank[:], axis=AX.X, op=ALU.max
+                    )
+            e_top = small.tile([P, JT], F32, tag="e_top")
+            nc.vector.tensor_reduce(out=e_top[:], in_=shared_top[:], axis=AX.X, op=ALU.max)
+            nc.vector.tensor_scalar_mul(out=e_top[:], in0=e_top[:], scalar1=RISE / SLOPE)
+            neg_shift = small.tile([P, JT * H], F32, tag="neg_shift")
+            for jt in range(JT):
+                neg_x = small.tile([P, H], F32, tag="neg_x")
+                nc.vector.tensor_scalar(
+                    out=neg_x[:], in0=a_top[:], scalar1=e_top[:, jt : jt + 1], scalar2=-1.0, op0=ALU.add, op1=ALU.mult
+                )
+                nc.vector.scalar_tensor_tensor(
+                    out=neg_shift[:, jt * H : (jt + 1) * H],
+                    in0=neg_x[:],
+                    scalar=SLOPE,
+                    in1=neg_x[:],
+                    op0=ALU.mult,
+                    op1=ALU.min,
+                )
+            return neg_shift
+
+        edges = [prepare_edges(0, chunk) for chunk in range(CHUNKS)]
+
+        with tc.tile_pool(name="vwork", bufs=2) as vwork:
+            wv_sb = vwork.tile([P, PACK, F_OUT], BF16, bufs=1)
+            nc.sync.dma_start(out=wv_sb[:], in_=Wv.rearrange("(t p) f -> p t f", p=P))
+            nf_sb = vwork.tile([P, ROW_TILES, F_IN], BF16, bufs=1)
+            nc.sync.dma_start(out=nf_sb[:], in_=node_features.rearrange("(jt p) c -> p jt c", p=P))
+
+            wv_grouped = vwork.tile([P, F_OUT, PACK], BF16, bufs=1, align_bytes=64)
+            nc.vector.tensor_copy(out=wv_grouped[:], in_=wv_sb[:].rearrange("p t f -> p f t"))
+            wv_codes = vwork.tile([P, F_OUT], U32, bufs=1, align_bytes=64)
+            wv_scales = vwork.tile([P, F_OUT], U8, bufs=1, align_bytes=64)
+            nc.vector.quantize_mx(
+                out=wv_codes[:].bitcast(FP8X4),
+                scales=wv_scales[:],
+                in_=wv_grouped[:].rearrange("p f t -> p (f t)"),
+            )
+
+            for g in range(PASSES):
+                nf_grouped = vwork.tile([P, PACK, P, PACK], BF16, align_bytes=64)
+                for t in range(PACK):
+                    nf_t_ps = psum.tile([P, PACK, P], BF16, tag="bank")
+                    for s in range(PACK):
+                        nc.tensor.transpose(
+                            out=nf_t_ps[:, s, :],
+                            in_=nf_sb[:, g * PACK + t, s * P : (s + 1) * P],
+                            identity=ident_b[:],
+                        )
+                    nc.scalar.copy(out=nf_grouped[:, t, :, :], in_=nf_t_ps[:].rearrange("p s r -> p r s"))
+                nf_codes = vwork.tile([P, PACK * P], U32, align_bytes=64)
+                nf_scales = vwork.tile([P, PACK * P], U8, align_bytes=64)
+                nc.vector.quantize_mx(
+                    out=nf_codes[:].bitcast(FP8X4),
+                    scales=nf_scales[:],
+                    in_=nf_grouped[:].rearrange("p t r s -> p (t r s)"),
+                )
+                v_planes = vwork.tile([P, PACK, F_OUT], BF16)
+                for t in range(PACK):
+                    v_ps = psum.tile([P, F_OUT], F32, tag="bank")
+                    nc.tensor.matmul_mx(
+                        out=v_ps[:],
+                        lhsT=nf_codes[:, t * P : (t + 1) * P].bitcast(FP8X4),
+                        lhsT_scale=nf_scales[:, t * P : (t + 1) * P],
+                        rhs=wv_codes[:].bitcast(FP8X4),
+                        rhs_scale=wv_scales[:],
+                        start=True,
+                        stop=True,
+                    )
+                    nc.scalar.activation(
+                        out=v_planes[:, t, :], in_=v_ps[:], func=ACT.Copy, scale=1.0 / math.sqrt(F_IN)
+                    )
+                v_grouped = vwork.tile([P, F_OUT, PACK], BF16, align_bytes=64)
+                nc.vector.tensor_copy(out=v_grouped[:], in_=v_planes[:].rearrange("p t f -> p f t"))
+                nc.vector.quantize_mx(
+                    out=v_codes[:, g, :].bitcast(FP8X4),
+                    scales=v_scales[:, g, :],
+                    in_=v_grouped[:].rearrange("p f t -> p (f t)"),
+                )
+
+        with tc.tile_pool(name="work", bufs=2, reuse_waits="tile") as work:
+
+            def exponentials(e_and_shared, neg_shift, h):
+                weights = work.tile([P, JT, N], F32, tag="weights")
+                sums = small.tile([P, JT, CHUNKS], F32, tag="sums")
+                for chunk in range(CHUNKS):
+                    e_t, shared_t = e_and_shared[chunk]
+                    head_t = work.tile([P, CB * PANEL], F32, tag="head", bufs=3)
+                    for b in range(CB):
+                        col = (chunk * CB + b) * H + h
+                        nc.vector.tensor_scalar(
+                            out=head_t[:, b * PANEL : (b + 1) * PANEL],
+                            in0=e_t[:, b * PANEL : (b + 1) * PANEL],
+                            scalar1=neg_a[:, col : col + 1],
+                            scalar2=a_over_rise[:, col : col + 1],
+                            op0=ALU.max,
+                            op1=ALU.add,
+                        )
+                    for jt in range(JT):
+                        bank = psum.tile([P, BANK], F32, tag="bank")
+                        for b in range(CB):
+                            nc.tensor.matmul(
+                                out=bank[:, b * P : (b + 1) * P],
+                                lhsT=block(head_t, b, jt),
+                                rhs=ident_f[:],
+                                is_transpose=True,
+                                start=True,
+                                stop=False,
+                            )
+                            nc.tensor.matmul(
+                                out=bank[:, b * P : (b + 1) * P],
+                                lhsT=block(shared_t, b, jt),
+                                rhs=ident_f[:],
+                                is_transpose=True,
+                                start=False,
+                                stop=True,
+                            )
+                        nc.scalar.activation(
+                            out=weights[:, jt, chunk * BANK : (chunk + 1) * BANK],
+                            in_=bank[:],
+                            func=ACT.Exp,
+                            bias=neg_shift[:, jt * H + h : jt * H + h + 1],
+                            scale=RISE,
+                            accum_out=sums[:, jt, chunk : chunk + 1],
+                        )
+                return weights, sums
+
+            def add_head(attn_sum, first_plane, weights, sums, h):
+                total = small.tile([P, JT], F32, tag="total")
+                nc.vector.tensor_reduce(out=total[:], in_=sums[:], axis=AX.X, op=ALU.add)
+                inverse = small.tile([P, JT], F32, tag="inverse")
+                nc.vector.reciprocal(out=inverse[:], in_=total[:])
+                for jt in range(JT):
+                    plane = attn_sum[:, first_plane + jt, :]
+                    if h == 0:
+                        nc.scalar.activation(
+                            out=plane, in_=weights[:, jt, :], func=ACT.Copy, scale=inverse[:, jt : jt + 1]
+                        )
+                    else:
+                        nc.vector.scalar_tensor_tensor(
+                            out=plane,
+                            in0=weights[:, jt, :],
+                            scalar=inverse[:, jt : jt + 1],
+                            in1=plane,
+                            op0=ALU.mult,
+                            op1=ALU.add,
+                        )
+
+            def quantise_attention(attn_sum, g):
+                for chunk in range(CHUNKS):
+                    cols = slice(chunk * BANK, (chunk + 1) * BANK)
+                    grouped = work.tile([P, BANK, PACK], BF16, tag="grouped", align_bytes=64)
+                    nc.scalar.activation(
+                        out=grouped[:],
+                        in_=attn_sum[:, :, cols].rearrange("p t i -> p i t"),
+                        func=ACT.Copy,
+                        scale=1.0 / H,
+                    )
+                    nc.vector.quantize_mx(
+                        out=attn_codes[:, g, cols].bitcast(FP8X4),
+                        scales=attn_scales[:, g, cols],
+                        in_=grouped[:].rearrange("p i t -> p (i t)"),
+                    )
+
+            attn_sum = None
+            for panel in range(PANELS):
+                g = panel // (PACK // JT)
+                first_plane = (panel % (PACK // JT)) * JT
+                if first_plane == 0:
+                    attn_sum = keep.tile([P, PACK, N], F32, tag="attn_sum")
+                neg_shift = softmax_shifts([shared_t for e_t, shared_t in edges])
+                next_edges = []
+                waiting = None
+                for h in range(H):
+                    done = exponentials(edges, neg_shift, h)
+                    if waiting is not None:
+                        add_head(attn_sum, first_plane, waiting[0], waiting[1], h - 1)
+                    waiting = done
+                    if panel + 1 < PANELS and h in (H - 3, H - 2):
+                        next_edges.append(prepare_edges(panel + 1, len(next_edges)))
+                if panel + 1 < PANELS:
+                    while len(next_edges) < CHUNKS:
+                        next_edges.append(prepare_edges(panel + 1, len(next_edges)))
+                add_head(attn_sum, first_plane, waiting[0], waiting[1], H - 1)
+                if first_plane + JT == PACK:
+                    quantise_attention(attn_sum, g)
+                edges = next_edges
+
+            for it in range(ROW_TILES):
+                rows = slice(it * P, (it + 1) * P)
+                out_ps = psum.tile([P, F_OUT], F32, tag="bank")
+                for g in range(PASSES):
+                    nc.tensor.matmul_mx(
+                        out=out_ps[:],
+                        lhsT=attn_codes[:, g, rows].bitcast(FP8X4),
+                        lhsT_scale=attn_scales[:, g, rows],
+                        rhs=v_codes[:, g, :].bitcast(FP8X4),
+                        rhs_scale=v_scales[:, g, :],
+                        start=(g == 0),
+                        stop=(g == PASSES - 1),
+                    )
+                exp_t = work.tile([P, F_OUT], F32, tag="exp")
+                nc.scalar.activation(out=exp_t[:], in_=out_ps[:], func=ACT.Exp)
+                line_t = work.tile([P, F_OUT], F32, tag="line")
+                nc.vector.tensor_scalar(
+                    out=line_t[:], in0=out_ps[:], scalar1=0.0, scalar2=-1.0, op0=ALU.max, op1=ALU.add
+                )
+                result = work.tile([P, F_OUT], F32, tag="result")
+                nc.vector.scalar_tensor_tensor(
+                    out=result[:], in0=exp_t[:], scalar=1.0, in1=line_t[:], op0=ALU.min, op1=ALU.add
+                )
+                nc.sync.dma_start(out=out_rows[:, it, :], in_=result[:])

@@ -33,6 +33,7 @@ PASSES = N // K_PASS
 JT = 2
 PANEL = JT * P
 PANELS = N // PANEL
+SUM_FIRST_EVERY = 3
 
 FLOPS = 2 * N * F_IN * F_OUT + 2 * N * N * F_OUT
 
@@ -93,6 +94,8 @@ def tile_egatlayer_pa_kernel(
         nc.vector.tensor_scalar_mul(out=neg_a[:], in0=q_plus_k[:], scalar1=-1.0 / math.sqrt(H))
         a_over_rise = const.tile([P, ROW_TILES * H], F32)
         nc.vector.tensor_scalar_mul(out=a_over_rise[:], in0=q_plus_k[:], scalar1=1.0 / (RISE * math.sqrt(H)))
+        a_slope_part = const.tile([P, ROW_TILES * H], F32)
+        nc.vector.tensor_scalar_mul(out=a_slope_part[:], in0=q_plus_k[:], scalar1=SLOPE / (RISE * math.sqrt(H)))
 
         a_t_ps = psum.tile([P, BANK], F32, tag="bank")
         nc.tensor.transpose(out=a_t_ps[:, :P], in_=a_sb[:], identity=ident_f[:])
@@ -119,7 +122,7 @@ def tile_egatlayer_pa_kernel(
         attn_codes = keep.tile([P, PASSES, N], U32, align_bytes=64)
         attn_scales = keep.tile([P, PASSES, N], U8, align_bytes=64)
 
-        def prepare_edges(panel, chunk):
+        def prepare_edges(panel, chunk, chunk_top):
             rows = slice(chunk * CB, (chunk + 1) * CB)
             cols = slice(panel * PANEL, (panel + 1) * PANEL)
             bond_t = stage.tile([P, CB * PANEL], BF16, tag="bond")
@@ -143,28 +146,32 @@ def tile_egatlayer_pa_kernel(
             nc.vector.scalar_tensor_tensor(
                 out=shared_t[:], in0=e_t[:], scalar=SLOPE / RISE, in1=mask_t[:], op0=ALU.mult, op1=ALU.add
             )
+            nc.vector.tensor_reduce(
+                out=chunk_top[:, chunk, :],
+                in_=shared_t[:].rearrange("p (b j) -> p j b", b=CB),
+                axis=AX.X,
+                op=ALU.max,
+            )
             return e_t, shared_t
 
         def block(tile_ap, b, jt):
             start = b * PANEL + jt * P
             return tile_ap[:, start : start + P]
 
-        def softmax_shifts(shared_tiles):
-            shared_top = small.tile([P, JT, CHUNKS], F32, tag="shared_top")
-            for chunk in range(CHUNKS):
-                for jt in range(JT):
-                    bank = psum.tile([P, BANK], F32, tag="bank")
-                    for b in range(CB):
-                        nc.tensor.transpose(
-                            out=bank[:, b * P : (b + 1) * P],
-                            in_=block(shared_tiles[chunk], b, jt),
-                            identity=ident_f[:],
-                        )
-                    nc.vector.tensor_reduce(
-                        out=shared_top[:, jt, chunk : chunk + 1], in_=bank[:], axis=AX.X, op=ALU.max
-                    )
+        def softmax_shifts(chunk_top):
+            panel_top = stage.tile([P, PANEL], F32, tag="panel_top")
+            nc.vector.tensor_reduce(
+                out=panel_top[:], in_=chunk_top[:].rearrange("p c j -> p j c"), axis=AX.X, op=ALU.max
+            )
+            bank = psum.tile([P, BANK], F32, tag="bank")
+            for jt in range(JT):
+                nc.tensor.transpose(
+                    out=bank[:, jt * P : (jt + 1) * P], in_=panel_top[:, jt * P : (jt + 1) * P], identity=ident_f[:]
+                )
             e_top = small.tile([P, JT], F32, tag="e_top")
-            nc.vector.tensor_reduce(out=e_top[:], in_=shared_top[:], axis=AX.X, op=ALU.max)
+            nc.vector.tensor_reduce(
+                out=e_top[:], in_=bank[:, : JT * P].rearrange("p (jt i) -> p jt i", jt=JT), axis=AX.X, op=ALU.max
+            )
             nc.vector.tensor_scalar_mul(out=e_top[:], in0=e_top[:], scalar1=RISE / SLOPE)
             neg_shift = small.tile([P, JT * H], F32, tag="neg_shift")
             for jt in range(JT):
@@ -182,7 +189,8 @@ def tile_egatlayer_pa_kernel(
                 )
             return neg_shift
 
-        edges = [prepare_edges(0, chunk) for chunk in range(CHUNKS)]
+        chunk_top = stage.tile([P, CHUNKS, PANEL], F32, tag="chunk_top")
+        edges = [prepare_edges(0, chunk, chunk_top) for chunk in range(CHUNKS)]
 
         with tc.tile_pool(name="vwork", bufs=2) as vwork:
             wv_sb = vwork.tile([P, PACK, F_OUT], BF16, bufs=1)
@@ -246,38 +254,60 @@ def tile_egatlayer_pa_kernel(
             def exponentials(e_and_shared, neg_shift, h):
                 weights = work.tile([P, JT, N], F32, tag="weights")
                 sums = small.tile([P, JT, CHUNKS], F32, tag="sums")
+                sum_first = h % SUM_FIRST_EVERY == 1
                 for chunk in range(CHUNKS):
                     e_t, shared_t = e_and_shared[chunk]
                     head_t = work.tile([P, CB * PANEL], F32, tag="head", bufs=3)
+                    if sum_first:
+                        relu_t = work.tile([P, CB * PANEL], F32, tag="relu")
                     for b in range(CB):
                         col = (chunk * CB + b) * H + h
-                        nc.vector.tensor_scalar(
-                            out=head_t[:, b * PANEL : (b + 1) * PANEL],
-                            in0=e_t[:, b * PANEL : (b + 1) * PANEL],
-                            scalar1=neg_a[:, col : col + 1],
-                            scalar2=a_over_rise[:, col : col + 1],
-                            op0=ALU.max,
-                            op1=ALU.add,
-                        )
+                        cols = slice(b * PANEL, (b + 1) * PANEL)
+                        if sum_first:
+                            nc.scalar.activation(
+                                out=relu_t[:, cols], in_=e_t[:, cols], func=ACT.Relu, bias=a_sb[:, col : col + 1]
+                            )
+                            nc.vector.scalar_tensor_tensor(
+                                out=head_t[:, cols],
+                                in0=relu_t[:, cols],
+                                scalar=a_slope_part[:, col : col + 1],
+                                in1=shared_t[:, cols],
+                                op0=ALU.add,
+                                op1=ALU.add,
+                            )
+                        else:
+                            nc.vector.tensor_scalar(
+                                out=head_t[:, cols],
+                                in0=e_t[:, cols],
+                                scalar1=neg_a[:, col : col + 1],
+                                scalar2=a_over_rise[:, col : col + 1],
+                                op0=ALU.max,
+                                op1=ALU.add,
+                            )
                     for jt in range(JT):
                         bank = psum.tile([P, BANK], F32, tag="bank")
                         for b in range(CB):
-                            nc.tensor.matmul(
-                                out=bank[:, b * P : (b + 1) * P],
-                                lhsT=block(head_t, b, jt),
-                                rhs=ident_f[:],
-                                is_transpose=True,
-                                start=True,
-                                stop=False,
-                            )
-                            nc.tensor.matmul(
-                                out=bank[:, b * P : (b + 1) * P],
-                                lhsT=block(shared_t, b, jt),
-                                rhs=ident_f[:],
-                                is_transpose=True,
-                                start=False,
-                                stop=True,
-                            )
+                            if sum_first:
+                                nc.tensor.transpose(
+                                    out=bank[:, b * P : (b + 1) * P], in_=block(head_t, b, jt), identity=ident_f[:]
+                                )
+                            else:
+                                nc.tensor.matmul(
+                                    out=bank[:, b * P : (b + 1) * P],
+                                    lhsT=block(head_t, b, jt),
+                                    rhs=ident_f[:],
+                                    is_transpose=True,
+                                    start=True,
+                                    stop=False,
+                                )
+                                nc.tensor.matmul(
+                                    out=bank[:, b * P : (b + 1) * P],
+                                    lhsT=block(shared_t, b, jt),
+                                    rhs=ident_f[:],
+                                    is_transpose=True,
+                                    start=False,
+                                    stop=True,
+                                )
                         nc.scalar.activation(
                             out=weights[:, jt, chunk * BANK : (chunk + 1) * BANK],
                             in_=bank[:],
@@ -331,8 +361,10 @@ def tile_egatlayer_pa_kernel(
                 first_plane = (panel % (PACK // JT)) * JT
                 if first_plane == 0:
                     attn_sum = keep.tile([P, PACK, N], F32, tag="attn_sum")
-                neg_shift = softmax_shifts([shared_t for e_t, shared_t in edges])
+                neg_shift = softmax_shifts(chunk_top)
                 next_edges = []
+                if panel + 1 < PANELS:
+                    chunk_top = stage.tile([P, CHUNKS, PANEL], F32, tag="chunk_top")
                 waiting = None
                 for h in range(H):
                     done = exponentials(edges, neg_shift, h)
@@ -340,15 +372,16 @@ def tile_egatlayer_pa_kernel(
                         add_head(attn_sum, first_plane, waiting[0], waiting[1], h - 1)
                     waiting = done
                     if panel + 1 < PANELS and h in (H - 3, H - 2):
-                        next_edges.append(prepare_edges(panel + 1, len(next_edges)))
+                        next_edges.append(prepare_edges(panel + 1, len(next_edges), chunk_top))
                 if panel + 1 < PANELS:
                     while len(next_edges) < CHUNKS:
-                        next_edges.append(prepare_edges(panel + 1, len(next_edges)))
+                        next_edges.append(prepare_edges(panel + 1, len(next_edges), chunk_top))
                 add_head(attn_sum, first_plane, waiting[0], waiting[1], H - 1)
                 if first_plane + JT == PACK:
                     quantise_attention(attn_sum, g)
                 edges = next_edges
 
+        with tc.tile_pool(name="finish", bufs=2, reuse_waits="tile") as finish:
             for it in range(ROW_TILES):
                 rows = slice(it * P, (it + 1) * P)
                 out_ps = psum.tile([P, F_OUT], F32, tag="bank")
@@ -362,13 +395,13 @@ def tile_egatlayer_pa_kernel(
                         start=(g == 0),
                         stop=(g == PASSES - 1),
                     )
-                exp_t = work.tile([P, F_OUT], F32, tag="exp")
+                exp_t = finish.tile([P, F_OUT], F32)
                 nc.scalar.activation(out=exp_t[:], in_=out_ps[:], func=ACT.Exp)
-                line_t = work.tile([P, F_OUT], F32, tag="line")
+                line_t = finish.tile([P, F_OUT], F32)
                 nc.vector.tensor_scalar(
                     out=line_t[:], in0=out_ps[:], scalar1=0.0, scalar2=-1.0, op0=ALU.max, op1=ALU.add
                 )
-                result = work.tile([P, F_OUT], F32, tag="result")
+                result = finish.tile([P, F_OUT], F32)
                 nc.vector.scalar_tensor_tensor(
                     out=result[:], in0=exp_t[:], scalar=1.0, in1=line_t[:], op0=ALU.min, op1=ALU.add
                 )

@@ -17,6 +17,7 @@ P = 128
 PACK = 4
 K_PASS = P * PACK
 BANK = 512
+PSUM_BANKS = 8
 
 N = 2048
 F_IN = 512
@@ -33,7 +34,6 @@ PASSES = N // K_PASS
 JT = 2
 PANEL = JT * P
 PANELS = N // PANEL
-SUM_FIRST_EVERY = 3
 
 FLOPS = 2 * N * F_IN * F_OUT + 2 * N * N * F_OUT
 
@@ -61,10 +61,10 @@ def tile_egatlayer_pa_kernel(
     with ExitStack() as ctx:
         const = ctx.enter_context(tc.tile_pool(name="const", bufs=1))
         keep = ctx.enter_context(tc.tile_pool(name="keep", bufs=1))
-        edge = ctx.enter_context(tc.tile_pool(name="edge", bufs=6))
+        edge = ctx.enter_context(tc.tile_pool(name="edge", bufs=2 * CHUNKS))
         stage = ctx.enter_context(tc.tile_pool(name="stage", bufs=2))
         small = ctx.enter_context(tc.tile_pool(name="small", bufs=3))
-        psum = ctx.enter_context(tc.psum_pool(name="psum", bufs=8))
+        psum = ctx.enter_context(tc.psum_pool(name="psum", bufs=PSUM_BANKS))
 
         ident_f = const.tile([P, P], F32)
         make_identity(nc, ident_f[:])
@@ -94,8 +94,6 @@ def tile_egatlayer_pa_kernel(
         nc.vector.tensor_scalar_mul(out=neg_a[:], in0=q_plus_k[:], scalar1=-1.0 / math.sqrt(H))
         a_over_rise = const.tile([P, ROW_TILES * H], F32)
         nc.vector.tensor_scalar_mul(out=a_over_rise[:], in0=q_plus_k[:], scalar1=1.0 / (RISE * math.sqrt(H)))
-        a_slope_part = const.tile([P, ROW_TILES * H], F32)
-        nc.vector.tensor_scalar_mul(out=a_slope_part[:], in0=q_plus_k[:], scalar1=SLOPE / (RISE * math.sqrt(H)))
 
         a_t_ps = psum.tile([P, BANK], F32, tag="bank")
         nc.tensor.transpose(out=a_t_ps[:, :P], in_=a_sb[:], identity=ident_f[:])
@@ -132,15 +130,14 @@ def tile_egatlayer_pa_kernel(
                 nc.sync.dma_start(
                     out=sb[:].rearrange("p (b j) -> p b j", b=CB), in_=rows_view[:, rows, cols]
                 )
-            gauss_t = stage.tile([P, CB * PANEL], F32, tag="gauss")
-            nc.scalar.activation(out=gauss_t[:], in_=dist_t[:], func=ACT.Copy, scale=gauss_weight[:, 0:1])
+            e_t = edge.tile([P, CB * PANEL], F32, tag="e")
+            nc.scalar.activation(out=e_t[:], in_=dist_t[:], func=ACT.Copy, scale=gauss_weight[:, 0:1])
             mask_t = stage.tile([P, CB * PANEL], BF16, tag="mask")
             nc.vector.tensor_scalar(
                 out=mask_t[:], in0=degree_t[:], scalar1=0.0, scalar2=NO_EDGE / RISE, op0=ALU.is_le, op1=ALU.mult
             )
-            e_t = edge.tile([P, CB * PANEL], F32, tag="e")
             nc.vector.scalar_tensor_tensor(
-                out=e_t[:], in0=bond_t[:], scalar=bond_weight[:, 0:1], in1=gauss_t[:], op0=ALU.mult, op1=ALU.add
+                out=e_t[:], in0=bond_t[:], scalar=bond_weight[:, 0:1], in1=e_t[:], op0=ALU.mult, op1=ALU.add
             )
             shared_t = edge.tile([P, CB * PANEL], F32, tag="shared")
             nc.vector.scalar_tensor_tensor(
@@ -159,7 +156,7 @@ def tile_egatlayer_pa_kernel(
             return tile_ap[:, start : start + P]
 
         def softmax_shifts(chunk_top):
-            panel_top = stage.tile([P, PANEL], F32, tag="panel_top")
+            panel_top = stage.tile([P, PANEL], F32, tag="panel_top", bufs=1)
             nc.vector.tensor_reduce(
                 out=panel_top[:], in_=chunk_top[:].rearrange("p c j -> p j c"), axis=AX.X, op=ALU.max
             )
@@ -189,14 +186,14 @@ def tile_egatlayer_pa_kernel(
                 )
             return neg_shift
 
-        chunk_top = stage.tile([P, CHUNKS, PANEL], F32, tag="chunk_top")
-        edges = [prepare_edges(0, chunk, chunk_top) for chunk in range(CHUNKS)]
-
         with tc.tile_pool(name="vwork", bufs=2) as vwork:
             wv_sb = vwork.tile([P, PACK, F_OUT], BF16, bufs=1)
             nc.sync.dma_start(out=wv_sb[:], in_=Wv.rearrange("(t p) f -> p t f", p=P))
             nf_sb = vwork.tile([P, ROW_TILES, F_IN], BF16, bufs=1)
             nc.sync.dma_start(out=nf_sb[:], in_=node_features.rearrange("(jt p) c -> p jt c", p=P))
+
+            chunk_top = stage.tile([P, CHUNKS, PANEL], F32, tag="chunk_top", bufs=1)
+            edges = [prepare_edges(0, chunk, chunk_top) for chunk in range(CHUNKS)]
 
             wv_grouped = vwork.tile([P, F_OUT, PACK], BF16, bufs=1, align_bytes=64)
             nc.vector.tensor_copy(out=wv_grouped[:], in_=wv_sb[:].rearrange("p t f -> p f t"))
@@ -254,60 +251,38 @@ def tile_egatlayer_pa_kernel(
             def exponentials(e_and_shared, neg_shift, h):
                 weights = work.tile([P, JT, N], F32, tag="weights")
                 sums = small.tile([P, JT, CHUNKS], F32, tag="sums")
-                sum_first = h % SUM_FIRST_EVERY == 1
                 for chunk in range(CHUNKS):
                     e_t, shared_t = e_and_shared[chunk]
-                    head_t = work.tile([P, CB * PANEL], F32, tag="head", bufs=3)
-                    if sum_first:
-                        relu_t = work.tile([P, CB * PANEL], F32, tag="relu")
+                    head_t = work.tile([P, CB * PANEL], F32, tag="head", bufs=4)
                     for b in range(CB):
                         col = (chunk * CB + b) * H + h
-                        cols = slice(b * PANEL, (b + 1) * PANEL)
-                        if sum_first:
-                            nc.scalar.activation(
-                                out=relu_t[:, cols], in_=e_t[:, cols], func=ACT.Relu, bias=a_sb[:, col : col + 1]
-                            )
-                            nc.vector.scalar_tensor_tensor(
-                                out=head_t[:, cols],
-                                in0=relu_t[:, cols],
-                                scalar=a_slope_part[:, col : col + 1],
-                                in1=shared_t[:, cols],
-                                op0=ALU.add,
-                                op1=ALU.add,
-                            )
-                        else:
-                            nc.vector.tensor_scalar(
-                                out=head_t[:, cols],
-                                in0=e_t[:, cols],
-                                scalar1=neg_a[:, col : col + 1],
-                                scalar2=a_over_rise[:, col : col + 1],
-                                op0=ALU.max,
-                                op1=ALU.add,
-                            )
+                        nc.vector.tensor_scalar(
+                            out=head_t[:, b * PANEL : (b + 1) * PANEL],
+                            in0=e_t[:, b * PANEL : (b + 1) * PANEL],
+                            scalar1=neg_a[:, col : col + 1],
+                            scalar2=a_over_rise[:, col : col + 1],
+                            op0=ALU.max,
+                            op1=ALU.add,
+                        )
                     for jt in range(JT):
                         bank = psum.tile([P, BANK], F32, tag="bank")
                         for b in range(CB):
-                            if sum_first:
-                                nc.tensor.transpose(
-                                    out=bank[:, b * P : (b + 1) * P], in_=block(head_t, b, jt), identity=ident_f[:]
-                                )
-                            else:
-                                nc.tensor.matmul(
-                                    out=bank[:, b * P : (b + 1) * P],
-                                    lhsT=block(head_t, b, jt),
-                                    rhs=ident_f[:],
-                                    is_transpose=True,
-                                    start=True,
-                                    stop=False,
-                                )
-                                nc.tensor.matmul(
-                                    out=bank[:, b * P : (b + 1) * P],
-                                    lhsT=block(shared_t, b, jt),
-                                    rhs=ident_f[:],
-                                    is_transpose=True,
-                                    start=False,
-                                    stop=True,
-                                )
+                            nc.tensor.matmul(
+                                out=bank[:, b * P : (b + 1) * P],
+                                lhsT=block(head_t, b, jt),
+                                rhs=ident_f[:],
+                                is_transpose=True,
+                                start=True,
+                                stop=False,
+                            )
+                            nc.tensor.matmul(
+                                out=bank[:, b * P : (b + 1) * P],
+                                lhsT=block(shared_t, b, jt),
+                                rhs=ident_f[:],
+                                is_transpose=True,
+                                start=False,
+                                stop=True,
+                            )
                         nc.scalar.activation(
                             out=weights[:, jt, chunk * BANK : (chunk + 1) * BANK],
                             in_=bank[:],
@@ -355,46 +330,58 @@ def tile_egatlayer_pa_kernel(
                         in_=grouped[:].rearrange("p i t -> p (i t)"),
                     )
 
-            attn_sum = None
-            for panel in range(PANELS):
-                g = panel // (PACK // JT)
+            def finish_head(attn_sum, panel, weights, sums, h):
                 first_plane = (panel % (PACK // JT)) * JT
-                if first_plane == 0:
-                    attn_sum = keep.tile([P, PACK, N], F32, tag="attn_sum")
+                add_head(attn_sum, first_plane, weights, sums, h)
+                if h == H - 1 and first_plane + JT == PACK:
+                    quantise_attention(attn_sum, panel // (PACK // JT))
+
+            attn_sum = None
+            waiting = None
+            for panel in range(PANELS):
+                first_plane = (panel % (PACK // JT)) * JT
                 neg_shift = softmax_shifts(chunk_top)
                 next_edges = []
                 if panel + 1 < PANELS:
-                    chunk_top = stage.tile([P, CHUNKS, PANEL], F32, tag="chunk_top")
-                waiting = None
+                    chunk_top = stage.tile([P, CHUNKS, PANEL], F32, tag="chunk_top", bufs=1)
                 for h in range(H):
-                    done = exponentials(edges, neg_shift, h)
+                    weights, sums = exponentials(edges, neg_shift, h)
                     if waiting is not None:
-                        add_head(attn_sum, first_plane, waiting[0], waiting[1], h - 1)
-                    waiting = done
-                    if panel + 1 < PANELS and h in (H - 3, H - 2):
+                        finish_head(*waiting)
+                    if h == 0 and first_plane == 0:
+                        attn_sum = keep.tile([P, PACK, N], F32, tag="attn_sum")
+                    waiting = (attn_sum, panel, weights, sums, h)
+                    if panel + 1 < PANELS and h % (H // CHUNKS) == 0:
                         next_edges.append(prepare_edges(panel + 1, len(next_edges), chunk_top))
-                if panel + 1 < PANELS:
-                    while len(next_edges) < CHUNKS:
-                        next_edges.append(prepare_edges(panel + 1, len(next_edges), chunk_top))
-                add_head(attn_sum, first_plane, waiting[0], waiting[1], H - 1)
-                if first_plane + JT == PACK:
-                    quantise_attention(attn_sum, g)
                 edges = next_edges
+            finish_head(*waiting)
 
         with tc.tile_pool(name="finish", bufs=2, reuse_waits="tile") as finish:
-            for it in range(ROW_TILES):
+            def out_pass(out_ps, it, g):
                 rows = slice(it * P, (it + 1) * P)
-                out_ps = psum.tile([P, F_OUT], F32, tag="bank")
-                for g in range(PASSES):
-                    nc.tensor.matmul_mx(
-                        out=out_ps[:],
-                        lhsT=attn_codes[:, g, rows].bitcast(FP8X4),
-                        lhsT_scale=attn_scales[:, g, rows],
-                        rhs=v_codes[:, g, :].bitcast(FP8X4),
-                        rhs_scale=v_scales[:, g, :],
-                        start=(g == 0),
-                        stop=(g == PASSES - 1),
-                    )
+                nc.tensor.matmul_mx(
+                    out=out_ps[:],
+                    lhsT=attn_codes[:, g, rows].bitcast(FP8X4),
+                    lhsT_scale=attn_scales[:, g, rows],
+                    rhs=v_codes[:, g, :].bitcast(FP8X4),
+                    rhs_scale=v_scales[:, g, :],
+                    start=(g == 0),
+                    stop=(g == PASSES - 1),
+                )
+
+            early = {}
+            for it in range(PSUM_BANKS):
+                early[it] = psum.tile([P, F_OUT], F32, tag="bank", name="out_ps")
+                for g in range(PASSES - 1):
+                    out_pass(early[it], it, g)
+            for it in range(ROW_TILES):
+                if it in early:
+                    out_ps = early[it]
+                else:
+                    out_ps = psum.tile([P, F_OUT], F32, tag="bank", name="out_ps")
+                    for g in range(PASSES - 1):
+                        out_pass(out_ps, it, g)
+                out_pass(out_ps, it, PASSES - 1)
                 exp_t = finish.tile([P, F_OUT], F32)
                 nc.scalar.activation(out=exp_t[:], in_=out_ps[:], func=ACT.Exp)
                 line_t = finish.tile([P, F_OUT], F32)

@@ -15,9 +15,9 @@ AX = mybir.AxisListType
 
 P = 128
 PACK = 4
+PAIR = 2
 K_PASS = P * PACK
 BANK = 512
-PSUM_BANKS = 8
 
 N = 2048
 F_IN = 512
@@ -34,6 +34,8 @@ PASSES = N // K_PASS
 JT = 2
 PANEL = JT * P
 PANELS = N // PANEL
+LAG = 3
+BASE = 0
 
 FLOPS = 2 * N * F_IN * F_OUT + 2 * N * N * F_OUT
 
@@ -57,19 +59,17 @@ def tile_egatlayer_pa_kernel(
     dist_rows = edges_features_distance.rearrange("(p it) j -> p it j", it=ROW_TILES)
     degree_rows = degree_matrix.rearrange("(p it) j -> p it j", it=ROW_TILES)
     out_rows = out.rearrange("(p it) f -> p it f", it=ROW_TILES)
+    nf_rows = node_features.rearrange("(g t p) c -> g p t c", t=PACK, p=P)
+    wv_rows = Wv.rearrange("(u p e) f -> p u (e f)", u=PAIR, p=P, e=PAIR)
 
     with ExitStack() as ctx:
         const = ctx.enter_context(tc.tile_pool(name="const", bufs=1))
         keep = ctx.enter_context(tc.tile_pool(name="keep", bufs=1))
         edge = ctx.enter_context(tc.tile_pool(name="edge", bufs=2 * CHUNKS))
         stage = ctx.enter_context(tc.tile_pool(name="stage", bufs=2))
-        small = ctx.enter_context(tc.tile_pool(name="small", bufs=3))
-        psum = ctx.enter_context(tc.psum_pool(name="psum", bufs=PSUM_BANKS))
-
-        ident_f = const.tile([P, P], F32)
-        make_identity(nc, ident_f[:])
-        ident_b = const.tile([P, P], BF16)
-        make_identity(nc, ident_b[:])
+        small = ctx.enter_context(tc.tile_pool(name="small", bufs=4))
+        work = ctx.enter_context(tc.tile_pool(name="work", bufs=2, reuse_waits="tile"))
+        psum = ctx.enter_context(tc.psum_pool(name="psum", bufs=8))
 
         w_bond_sb = const.tile([P, 1], BF16)
         nc.sync.dma_start(out=w_bond_sb[:], in_=w_bond.partition_broadcast(P))
@@ -77,23 +77,38 @@ def tile_egatlayer_pa_kernel(
         nc.sync.dma_start(out=w_contrib_sb[:], in_=w_bond_contrib.partition_broadcast(P))
         w_gauss_sb = const.tile([P, 1], BF16)
         nc.sync.dma_start(out=w_gauss_sb[:], in_=w_gauss.partition_broadcast(P))
+        q_sb = const.tile([P, ROW_TILES * H], BF16)
+        nc.sync.dma_start(out=q_sb[:], in_=q.rearrange("(p it) h -> p (it h)", it=ROW_TILES))
+        k_sb = const.tile([P, ROW_TILES * H], BF16)
+        nc.sync.dma_start(out=k_sb[:], in_=k.rearrange("(p it) h -> p (it h)", it=ROW_TILES))
+
+        ident_f = const.tile([P, P], F32)
+        make_identity(nc, ident_f[:])
+
         bond_weight = const.tile([P, 1], F32)
         nc.vector.tensor_tensor(out=bond_weight[:], in0=w_bond_sb[:], in1=w_contrib_sb[:], op=ALU.mult)
         gauss_weight = const.tile([P, 1], F32)
         nc.vector.tensor_copy(out=gauss_weight[:], in_=w_gauss_sb[:])
 
-        q_sb = const.tile([P, ROW_TILES * H], BF16)
-        nc.sync.dma_start(out=q_sb[:], in_=q.rearrange("(p it) h -> p (it h)", it=ROW_TILES))
-        k_sb = const.tile([P, ROW_TILES * H], BF16)
-        nc.sync.dma_start(out=k_sb[:], in_=k.rearrange("(p it) h -> p (it h)", it=ROW_TILES))
         q_plus_k = const.tile([P, ROW_TILES * H], F32)
         nc.vector.tensor_tensor(out=q_plus_k[:], in0=q_sb[:], in1=k_sb[:], op=ALU.add)
+        by_head = q_plus_k[:].rearrange("p (it h) -> p it h", h=H)
+        base_a = const.tile([P, ROW_TILES], F32)
+        nc.vector.tensor_scalar_mul(out=base_a[:], in0=by_head[:, :, BASE], scalar1=1.0 / math.sqrt(H))
+        d_raw = const.tile([P, ROW_TILES, H], F32)
+        nc.vector.tensor_tensor(
+            out=d_raw[:],
+            in0=by_head,
+            in1=by_head[:, :, BASE : BASE + 1].to_broadcast([P, ROW_TILES, H]),
+            op=ALU.subtract,
+        )
+        d_flat = d_raw[:].rearrange("p it h -> p (it h)")
         a_sb = const.tile([P, ROW_TILES * H], F32)
-        nc.vector.tensor_scalar_mul(out=a_sb[:], in0=q_plus_k[:], scalar1=1.0 / math.sqrt(H))
+        nc.vector.tensor_scalar_mul(out=a_sb[:], in0=d_flat, scalar1=1.0 / math.sqrt(H))
         neg_a = const.tile([P, ROW_TILES * H], F32)
-        nc.vector.tensor_scalar_mul(out=neg_a[:], in0=q_plus_k[:], scalar1=-1.0 / math.sqrt(H))
+        nc.vector.tensor_scalar_mul(out=neg_a[:], in0=d_flat, scalar1=-1.0 / math.sqrt(H))
         a_over_rise = const.tile([P, ROW_TILES * H], F32)
-        nc.vector.tensor_scalar_mul(out=a_over_rise[:], in0=q_plus_k[:], scalar1=1.0 / (RISE * math.sqrt(H)))
+        nc.vector.tensor_scalar_mul(out=a_over_rise[:], in0=d_flat, scalar1=1.0 / (RISE * math.sqrt(H)))
 
         a_t_ps = psum.tile([P, BANK], F32, tag="bank")
         nc.tensor.transpose(out=a_t_ps[:, :P], in_=a_sb[:], identity=ident_f[:])
@@ -107,94 +122,122 @@ def tile_egatlayer_pa_kernel(
             start=True,
             stop=True,
         )
-        a_top = const.tile([P, H], F32)
+        a_top = const.tile([P, 1, H], F32)
         nc.vector.tensor_reduce(
-            out=a_top[:],
+            out=a_top[:, 0, :],
             in_=a_spread_ps[:, :P].rearrange("p (it h) -> p h it", h=H),
             axis=AX.X,
             op=ALU.max,
         )
+        neg_a_top = const.tile([P, 1, H], F32)
+        nc.vector.tensor_scalar_mul(out=neg_a_top[:, 0, :], in0=a_top[:, 0, :], scalar1=-1.0)
 
         v_codes = keep.tile([P, PASSES, F_OUT], U32, align_bytes=64)
         v_scales = keep.tile([P, PASSES, F_OUT], U8, align_bytes=64)
-        attn_codes = keep.tile([P, PASSES, N], U32, align_bytes=64)
-        attn_scales = keep.tile([P, PASSES, N], U8, align_bytes=64)
 
-        def prepare_edges(panel, chunk, chunk_top):
+        def new_panel(panel):
+            return {
+                "panel": panel,
+                "top": stage.tile([P, CHUNKS, PANEL], F32, tag="chunk_top", bufs=1, name="chunk_top"),
+                "e": [],
+                "shared": [],
+                "loads": [],
+            }
+
+        def load_edges(st, chunk):
             rows = slice(chunk * CB, (chunk + 1) * CB)
-            cols = slice(panel * PANEL, (panel + 1) * PANEL)
-            bond_t = stage.tile([P, CB * PANEL], BF16, tag="bond")
-            dist_t = stage.tile([P, CB * PANEL], BF16, tag="dist")
-            degree_t = stage.tile([P, CB * PANEL], BF16, tag="degree")
-            for sb, rows_view in ((bond_t, bond_rows), (dist_t, dist_rows), (degree_t, degree_rows)):
-                nc.sync.dma_start(
-                    out=sb[:].rearrange("p (b j) -> p b j", b=CB), in_=rows_view[:, rows, cols]
-                )
+            cols = slice(st["panel"] * PANEL, (st["panel"] + 1) * PANEL)
+            tiles = []
+            for tag, rows_view in (("dist", dist_rows), ("bond", bond_rows), ("degree", degree_rows)):
+                t = stage.tile([P, CB * PANEL], BF16, tag=tag, name="load_t")
+                nc.sync.dma_start(out=t[:].rearrange("p (b j) -> p b j", b=CB), in_=rows_view[:, rows, cols])
+                tiles.append(t)
+            st["loads"].append(tiles)
+
+        def scale_dist(st, chunk):
             e_t = edge.tile([P, CB * PANEL], F32, tag="e")
-            nc.scalar.activation(out=e_t[:], in_=dist_t[:], func=ACT.Copy, scale=gauss_weight[:, 0:1])
-            mask_t = stage.tile([P, CB * PANEL], BF16, tag="mask")
+            for b in range(CB):
+                it = chunk * CB + b
+                nc.scalar.activation(
+                    out=e_t[:, b * PANEL : (b + 1) * PANEL],
+                    in_=st["loads"][chunk][0][:, b * PANEL : (b + 1) * PANEL],
+                    func=ACT.Identity,
+                    scale=gauss_weight[:, 0:1],
+                    bias=base_a[:, it : it + 1],
+                )
+            st["e"].append(e_t)
+
+        def make_mask(st, chunk):
+            degree_t = st["loads"][chunk][2]
             nc.vector.tensor_scalar(
-                out=mask_t[:], in0=degree_t[:], scalar1=0.0, scalar2=NO_EDGE / RISE, op0=ALU.is_le, op1=ALU.mult
+                out=degree_t[:], in0=degree_t[:], scalar1=0.0, scalar2=NO_EDGE / RISE, op0=ALU.is_le, op1=ALU.mult
             )
+
+        def add_bond(st, chunk):
+            e_t = st["e"][chunk]
             nc.vector.scalar_tensor_tensor(
-                out=e_t[:], in0=bond_t[:], scalar=bond_weight[:, 0:1], in1=e_t[:], op0=ALU.mult, op1=ALU.add
+                out=e_t[:], in0=st["loads"][chunk][1][:], scalar=bond_weight[:, 0:1], in1=e_t[:],
+                op0=ALU.mult, op1=ALU.add,
             )
+
+        def make_shared(st, chunk):
             shared_t = edge.tile([P, CB * PANEL], F32, tag="shared")
             nc.vector.scalar_tensor_tensor(
-                out=shared_t[:], in0=e_t[:], scalar=SLOPE / RISE, in1=mask_t[:], op0=ALU.mult, op1=ALU.add
+                out=shared_t[:], in0=st["e"][chunk][:], scalar=SLOPE / RISE, in1=st["loads"][chunk][2][:],
+                op0=ALU.mult, op1=ALU.add,
             )
+            st["shared"].append(shared_t)
+
+        def reduce_shared(st, chunk):
             nc.vector.tensor_reduce(
-                out=chunk_top[:, chunk, :],
-                in_=shared_t[:].rearrange("p (b j) -> p j b", b=CB),
+                out=st["top"][:, chunk, :],
+                in_=st["shared"][chunk][:].rearrange("p (b j) -> p j b", b=CB),
                 axis=AX.X,
                 op=ALU.max,
             )
-            return e_t, shared_t
 
-        def block(tile_ap, b, jt):
-            start = b * PANEL + jt * P
-            return tile_ap[:, start : start + P]
-
-        def softmax_shifts(chunk_top):
+        def panel_tops(st):
             panel_top = stage.tile([P, PANEL], F32, tag="panel_top", bufs=1)
             nc.vector.tensor_reduce(
-                out=panel_top[:], in_=chunk_top[:].rearrange("p c j -> p j c"), axis=AX.X, op=ALU.max
+                out=panel_top[:], in_=st["top"][:].rearrange("p c j -> p j c"), axis=AX.X, op=ALU.max
             )
-            bank = psum.tile([P, BANK], F32, tag="bank")
+            st["top_bank"] = psum.tile([P, BANK], F32, tag="bank", name="top_bank")
             for jt in range(JT):
                 nc.tensor.transpose(
-                    out=bank[:, jt * P : (jt + 1) * P], in_=panel_top[:, jt * P : (jt + 1) * P], identity=ident_f[:]
+                    out=st["top_bank"][:, jt * P : (jt + 1) * P],
+                    in_=panel_top[:, jt * P : (jt + 1) * P],
+                    identity=ident_f[:],
                 )
-            e_top = small.tile([P, JT], F32, tag="e_top")
+
+        def column_tops(st):
+            st["e_top"] = small.tile([P, JT, 1], F32, tag="e_top", name="e_top")
             nc.vector.tensor_reduce(
-                out=e_top[:], in_=bank[:, : JT * P].rearrange("p (jt i) -> p jt i", jt=JT), axis=AX.X, op=ALU.max
+                out=st["e_top"][:, :, 0],
+                in_=st["top_bank"][:, : JT * P].rearrange("p (jt i) -> p jt i", jt=JT),
+                axis=AX.X,
+                op=ALU.max,
             )
-            nc.vector.tensor_scalar_mul(out=e_top[:], in0=e_top[:], scalar1=RISE / SLOPE)
-            neg_shift = small.tile([P, JT * H], F32, tag="neg_shift")
-            for jt in range(JT):
-                neg_x = small.tile([P, H], F32, tag="neg_x")
-                nc.vector.tensor_scalar(
-                    out=neg_x[:], in0=a_top[:], scalar1=e_top[:, jt : jt + 1], scalar2=-1.0, op0=ALU.add, op1=ALU.mult
-                )
-                nc.vector.scalar_tensor_tensor(
-                    out=neg_shift[:, jt * H : (jt + 1) * H],
-                    in0=neg_x[:],
-                    scalar=SLOPE,
-                    in1=neg_x[:],
-                    op0=ALU.mult,
-                    op1=ALU.min,
-                )
-            return neg_shift
 
-        with tc.tile_pool(name="vwork", bufs=2) as vwork:
+        def negate_scores(st):
+            st["neg_x"] = small.tile([P, JT, H], F32, tag="neg_x", name="neg_x")
+            nc.vector.scalar_tensor_tensor(
+                out=st["neg_x"][:],
+                in0=st["e_top"][:].to_broadcast([P, JT, H]),
+                scalar=-RISE / SLOPE,
+                in1=neg_a_top[:].to_broadcast([P, JT, H]),
+                op0=ALU.mult,
+                op1=ALU.add,
+            )
+
+        def softmax_shifts(st):
+            st["neg_shift"] = small.tile([P, JT, H], F32, tag="neg_shift", name="neg_shift")
+            nc.vector.scalar_tensor_tensor(
+                out=st["neg_shift"][:], in0=st["neg_x"][:], scalar=SLOPE, in1=st["neg_x"][:], op0=ALU.mult, op1=ALU.min
+            )
+
+        def quantise_wv(vwork):
             wv_sb = vwork.tile([P, PACK, F_OUT], BF16, bufs=1)
-            nc.sync.dma_start(out=wv_sb[:], in_=Wv.rearrange("(t p) f -> p t f", p=P))
-            nf_sb = vwork.tile([P, ROW_TILES, F_IN], BF16, bufs=1)
-            nc.sync.dma_start(out=nf_sb[:], in_=node_features.rearrange("(jt p) c -> p jt c", p=P))
-
-            chunk_top = stage.tile([P, CHUNKS, PANEL], F32, tag="chunk_top", bufs=1)
-            edges = [prepare_edges(0, chunk, chunk_top) for chunk in range(CHUNKS)]
-
+            nc.sync.dma_start(out=wv_sb[:].rearrange("p (u e) f -> p u (e f)", u=PAIR), in_=wv_rows)
             wv_grouped = vwork.tile([P, F_OUT, PACK], BF16, bufs=1, align_bytes=64)
             nc.vector.tensor_copy(out=wv_grouped[:], in_=wv_sb[:].rearrange("p t f -> p f t"))
             wv_codes = vwork.tile([P, F_OUT], U32, bufs=1, align_bytes=64)
@@ -204,192 +247,255 @@ def tile_egatlayer_pa_kernel(
                 scales=wv_scales[:],
                 in_=wv_grouped[:].rearrange("p f t -> p (f t)"),
             )
+            return wv_codes, wv_scales
 
-            for g in range(PASSES):
-                nf_grouped = vwork.tile([P, PACK, P, PACK], BF16, align_bytes=64)
-                for t in range(PACK):
-                    nf_t_ps = psum.tile([P, PACK, P], BF16, tag="bank")
-                    for s in range(PACK):
+        def load_nodes(vwork, g):
+            nf_sb = vwork.tile([P, PACK, F_IN], BF16, tag="nf_sb", align_bytes=64)
+            nc.sync.dma_start(out=nf_sb[:], in_=nf_rows[g])
+            return nf_sb
+
+        def make_v(vwork, g, nf_sb, wv_codes, wv_scales):
+            nf_grouped = vwork.tile([P, PACK, P, PACK], BF16, bufs=1, align_bytes=64)
+            for half in range(PAIR):
+                words_ps = psum.tile([P, PAIR, PAIR, P], F32, tag="bank", name="words_ps")
+                for s in range(PAIR):
+                    words = nf_sb[:, PAIR * half + s, :].bitcast(F32)
+                    for u in range(PAIR):
                         nc.tensor.transpose(
-                            out=nf_t_ps[:, s, :],
-                            in_=nf_sb[:, g * PACK + t, s * P : (s + 1) * P],
-                            identity=ident_b[:],
+                            out=words_ps[:, s, u, :], in_=words[:, u * P : (u + 1) * P], identity=ident_f[:]
                         )
-                    nc.scalar.copy(out=nf_grouped[:, t, :, :], in_=nf_t_ps[:].rearrange("p s r -> p r s"))
-                nf_codes = vwork.tile([P, PACK * P], U32, align_bytes=64)
-                nf_scales = vwork.tile([P, PACK * P], U8, align_bytes=64)
-                nc.vector.quantize_mx(
-                    out=nf_codes[:].bitcast(FP8X4),
-                    scales=nf_scales[:],
-                    in_=nf_grouped[:].rearrange("p t r s -> p (t r s)"),
+                nc.scalar.copy(
+                    out=nf_grouped[:, PAIR * half : PAIR * (half + 1), :, :]
+                    .rearrange("p t r k -> p (t r k)")
+                    .bitcast(F32)
+                    .rearrange("p (t r u) -> p t r u", t=PAIR, u=PAIR),
+                    in_=words_ps[:].rearrange("p t u r -> p t r u"),
                 )
-                v_planes = vwork.tile([P, PACK, F_OUT], BF16)
-                for t in range(PACK):
-                    v_ps = psum.tile([P, F_OUT], F32, tag="bank")
-                    nc.tensor.matmul_mx(
-                        out=v_ps[:],
-                        lhsT=nf_codes[:, t * P : (t + 1) * P].bitcast(FP8X4),
-                        lhsT_scale=nf_scales[:, t * P : (t + 1) * P],
-                        rhs=wv_codes[:].bitcast(FP8X4),
-                        rhs_scale=wv_scales[:],
-                        start=True,
-                        stop=True,
+            nf_codes = vwork.tile([P, PACK * P], U32, align_bytes=64)
+            nf_scales = vwork.tile([P, PACK * P], U8, align_bytes=64)
+            nc.vector.quantize_mx(
+                out=nf_codes[:].bitcast(FP8X4),
+                scales=nf_scales[:],
+                in_=nf_grouped[:].rearrange("p t r s -> p (t r s)"),
+            )
+            v_planes = vwork.tile([P, PACK, F_OUT], BF16)
+            for t in range(PACK):
+                v_ps = psum.tile([P, F_OUT], F32, tag="bank")
+                nc.tensor.matmul_mx(
+                    out=v_ps[:],
+                    lhsT=nf_codes[:, t * P : (t + 1) * P].bitcast(FP8X4),
+                    lhsT_scale=nf_scales[:, t * P : (t + 1) * P],
+                    rhs=wv_codes[:].bitcast(FP8X4),
+                    rhs_scale=wv_scales[:],
+                    start=True,
+                    stop=True,
+                )
+                nc.scalar.activation(
+                    out=v_planes[:, t, :], in_=v_ps[:], func=ACT.Copy, scale=1.0 / math.sqrt(F_IN)
+                )
+            v_grouped = vwork.tile([P, F_OUT, PACK], BF16, align_bytes=64)
+            nc.vector.tensor_copy(out=v_grouped[:], in_=v_planes[:].rearrange("p t f -> p f t"))
+            nc.vector.quantize_mx(
+                out=v_codes[:, g, :].bitcast(FP8X4),
+                scales=v_scales[:, g, :],
+                in_=v_grouped[:].rearrange("p f t -> p (f t)"),
+            )
+
+        def new_head():
+            return {
+                "w": [work.tile([P, N], F32, tag="w", bufs=6, name="w") for jt in range(JT)],
+                "sums": small.tile([P, JT, CHUNKS], F32, tag="sums", name="sums"),
+            }
+
+        def exponentials(st, head, h, chunk):
+            e_t = st["e"][chunk]
+            shared_t = st["shared"][chunk]
+            head_t = work.tile([P, CB * PANEL], F32, tag="head", bufs=4)
+            if h == BASE:
+                nc.scalar.activation(out=head_t[:], in_=e_t[:], func=ACT.Relu)
+            else:
+                for b in range(CB):
+                    col = (chunk * CB + b) * H + h
+                    nc.vector.tensor_scalar(
+                        out=head_t[:, b * PANEL : (b + 1) * PANEL],
+                        in0=e_t[:, b * PANEL : (b + 1) * PANEL],
+                        scalar1=neg_a[:, col : col + 1],
+                        scalar2=a_over_rise[:, col : col + 1],
+                        op0=ALU.max,
+                        op1=ALU.add,
                     )
-                    nc.scalar.activation(
-                        out=v_planes[:, t, :], in_=v_ps[:], func=ACT.Copy, scale=1.0 / math.sqrt(F_IN)
+            for jt in range(JT):
+                bank = psum.tile([P, BANK], F32, tag="bank")
+                for b in range(CB):
+                    cols = slice(b * PANEL + jt * P, b * PANEL + (jt + 1) * P)
+                    nc.tensor.matmul(
+                        out=bank[:, b * P : (b + 1) * P], lhsT=head_t[:, cols], rhs=ident_f[:],
+                        is_transpose=True, start=True, stop=False,
                     )
-                v_grouped = vwork.tile([P, F_OUT, PACK], BF16, align_bytes=64)
-                nc.vector.tensor_copy(out=v_grouped[:], in_=v_planes[:].rearrange("p t f -> p f t"))
-                nc.vector.quantize_mx(
-                    out=v_codes[:, g, :].bitcast(FP8X4),
-                    scales=v_scales[:, g, :],
-                    in_=v_grouped[:].rearrange("p f t -> p (f t)"),
+                    nc.tensor.matmul(
+                        out=bank[:, b * P : (b + 1) * P], lhsT=shared_t[:, cols], rhs=ident_f[:],
+                        is_transpose=True, start=False, stop=True,
+                    )
+                nc.scalar.activation(
+                    out=head["w"][jt][:, chunk * BANK : (chunk + 1) * BANK],
+                    in_=bank[:],
+                    func=ACT.Exp,
+                    bias=st["neg_shift"][:, jt, h : h + 1],
+                    scale=RISE,
+                    accum_out=head["sums"][:, jt, chunk : chunk + 1],
                 )
 
-        with tc.tile_pool(name="work", bufs=2, reuse_waits="tile") as work:
+        def add_sums(head):
+            head["total"] = small.tile([P, JT], F32, tag="total", name="total")
+            nc.vector.tensor_reduce(out=head["total"][:], in_=head["sums"][:], axis=AX.X, op=ALU.add)
 
-            def exponentials(e_and_shared, neg_shift, h):
-                weights = work.tile([P, JT, N], F32, tag="weights")
-                sums = small.tile([P, JT, CHUNKS], F32, tag="sums")
+        def invert_sums(head):
+            head["inverse"] = small.tile([P, JT], F32, tag="inverse", name="inverse")
+            nc.vector.reciprocal(out=head["inverse"][:], in_=head["total"][:])
+
+        def add_head(panel, head, h, jt, cols):
+            if h == 0 and jt == 0 and panel % PAIR == 0:
+                state["attn_sum"] = keep.tile([P, PACK, N], F32, tag="attn_sum", name="attn_sum")
+            plane = state["attn_sum"][:, (panel % PAIR) * JT + jt, cols]
+            scale = head["inverse"][:, jt : jt + 1]
+            if h == 0:
+                nc.scalar.activation(out=plane, in_=head["w"][jt][:, cols], func=ACT.Copy, scale=scale)
+            else:
+                nc.vector.scalar_tensor_tensor(
+                    out=plane, in0=head["w"][jt][:, cols], scalar=scale, in1=plane, op0=ALU.mult, op1=ALU.add
+                )
+
+        def group_mean(g, chunk):
+            cols = slice(chunk * BANK, (chunk + 1) * BANK)
+            grouped = late.tile([P, BANK, PACK], BF16, tag="grouped", align_bytes=64, name="grouped")
+            nc.scalar.activation(
+                out=grouped[:],
+                in_=state["attn_sum"][:, :, cols].rearrange("p t i -> p i t"),
+                func=ACT.Copy,
+                scale=1.0 / H,
+            )
+            return grouped
+
+        def quantise_mean(g, chunk, grouped):
+            cols = slice(chunk * BANK, (chunk + 1) * BANK)
+            nc.vector.quantize_mx(
+                out=attn_codes[:, g, cols].bitcast(FP8X4),
+                scales=attn_scales[PACK * g :, cols],
+                in_=grouped[:].rearrange("p i t -> p (i t)"),
+            )
+
+        def mean_step(g, chunk):
+            quantise_mean(g, chunk, group_mean(g, chunk))
+
+        state = {"slot": 0}
+        schedule = {}
+
+        def at(slot, task):
+            schedule.setdefault(slot, []).append(task)
+
+        def run_slot():
+            for task in schedule.get(state["slot"], []):
+                task()
+            state["slot"] = state["slot"] + 1
+
+        def plan_head(panel, head, h, slot):
+            at(slot + LAG, lambda: add_sums(head))
+            at(slot + LAG + 1, lambda: invert_sums(head))
+            if panel == PANELS - 1 and h == H - 1:
                 for chunk in range(CHUNKS):
-                    e_t, shared_t = e_and_shared[chunk]
-                    head_t = work.tile([P, CB * PANEL], F32, tag="head", bufs=4)
-                    for b in range(CB):
-                        col = (chunk * CB + b) * H + h
-                        nc.vector.tensor_scalar(
-                            out=head_t[:, b * PANEL : (b + 1) * PANEL],
-                            in0=e_t[:, b * PANEL : (b + 1) * PANEL],
-                            scalar1=neg_a[:, col : col + 1],
-                            scalar2=a_over_rise[:, col : col + 1],
-                            op0=ALU.max,
-                            op1=ALU.add,
-                        )
                     for jt in range(JT):
-                        bank = psum.tile([P, BANK], F32, tag="bank")
-                        for b in range(CB):
-                            nc.tensor.matmul(
-                                out=bank[:, b * P : (b + 1) * P],
-                                lhsT=block(head_t, b, jt),
-                                rhs=ident_f[:],
-                                is_transpose=True,
-                                start=True,
-                                stop=False,
-                            )
-                            nc.tensor.matmul(
-                                out=bank[:, b * P : (b + 1) * P],
-                                lhsT=block(shared_t, b, jt),
-                                rhs=ident_f[:],
-                                is_transpose=True,
-                                start=False,
-                                stop=True,
-                            )
-                        nc.scalar.activation(
-                            out=weights[:, jt, chunk * BANK : (chunk + 1) * BANK],
-                            in_=bank[:],
-                            func=ACT.Exp,
-                            bias=neg_shift[:, jt * H + h : jt * H + h + 1],
-                            scale=RISE,
-                            accum_out=sums[:, jt, chunk : chunk + 1],
-                        )
-                return weights, sums
-
-            def add_head(attn_sum, first_plane, weights, sums, h):
-                total = small.tile([P, JT], F32, tag="total")
-                nc.vector.tensor_reduce(out=total[:], in_=sums[:], axis=AX.X, op=ALU.add)
-                inverse = small.tile([P, JT], F32, tag="inverse")
-                nc.vector.reciprocal(out=inverse[:], in_=total[:])
+                        at(slot + LAG + 2, lambda jt=jt, chunk=chunk: add_head(panel, head, h, jt, slice(chunk * BANK, (chunk + 1) * BANK)))
+                    at(slot + LAG + 2, lambda chunk=chunk: mean_step(panel // PAIR, chunk))
+            else:
                 for jt in range(JT):
-                    plane = attn_sum[:, first_plane + jt, :]
-                    if h == 0:
-                        nc.scalar.activation(
-                            out=plane, in_=weights[:, jt, :], func=ACT.Copy, scale=inverse[:, jt : jt + 1]
-                        )
-                    else:
-                        nc.vector.scalar_tensor_tensor(
-                            out=plane,
-                            in0=weights[:, jt, :],
-                            scalar=inverse[:, jt : jt + 1],
-                            in1=plane,
-                            op0=ALU.mult,
-                            op1=ALU.add,
-                        )
+                    at(slot + LAG + 2 + jt, lambda jt=jt: add_head(panel, head, h, jt, slice(0, N)))
+                if h == H - 1 and panel % PAIR == PAIR - 1:
+                    for chunk in range(CHUNKS):
+                        at(slot + LAG + 4 + chunk // 2, lambda chunk=chunk: mean_step(panel // PAIR, chunk))
 
-            def quantise_attention(attn_sum, g):
-                for chunk in range(CHUNKS):
-                    cols = slice(chunk * BANK, (chunk + 1) * BANK)
-                    grouped = work.tile([P, BANK, PACK], BF16, tag="grouped", align_bytes=64)
-                    nc.scalar.activation(
-                        out=grouped[:],
-                        in_=attn_sum[:, :, cols].rearrange("p t i -> p i t"),
-                        func=ACT.Copy,
-                        scale=1.0 / H,
-                    )
-                    nc.vector.quantize_mx(
-                        out=attn_codes[:, g, cols].bitcast(FP8X4),
-                        scales=attn_scales[:, g, cols],
-                        in_=grouped[:].rearrange("p i t -> p (i t)"),
-                    )
+        def plan_edges(st, slot):
+            for chunk in range(CHUNKS):
+                first = slot + 7 * chunk
+                at(first, lambda chunk=chunk: load_edges(st, chunk))
+                at(first + 2, lambda chunk=chunk: scale_dist(st, chunk))
+                at(first + 2, lambda chunk=chunk: make_mask(st, chunk))
+                at(first + 3, lambda chunk=chunk: add_bond(st, chunk))
+                at(first + 4, lambda chunk=chunk: make_shared(st, chunk))
+                at(first + 5, lambda chunk=chunk: reduce_shared(st, chunk))
+            at(slot + 27, lambda: panel_tops(st))
+            at(slot + 29, lambda: column_tops(st))
+            at(slot + 30, lambda: negate_scores(st))
+            at(slot + 31, lambda: softmax_shifts(st))
 
-            def finish_head(attn_sum, panel, weights, sums, h):
-                first_plane = (panel % (PACK // JT)) * JT
-                add_head(attn_sum, first_plane, weights, sums, h)
-                if h == H - 1 and first_plane + JT == PACK:
-                    quantise_attention(attn_sum, panel // (PACK // JT))
+        def run_head(st, h):
+            if h == 0 and st["panel"] + 1 < PANELS:
+                state["next"] = new_panel(st["panel"] + 1)
+                plan_edges(state["next"], state["slot"])
+            head = new_head()
+            for chunk in range(CHUNKS):
+                exponentials(st, head, h, chunk)
+                run_slot()
+            plan_head(st["panel"], head, h, state["slot"])
 
-            attn_sum = None
-            waiting = None
-            for panel in range(PANELS):
-                first_plane = (panel % (PACK // JT)) * JT
-                neg_shift = softmax_shifts(chunk_top)
-                next_edges = []
-                if panel + 1 < PANELS:
-                    chunk_top = stage.tile([P, CHUNKS, PANEL], F32, tag="chunk_top", bufs=1)
-                for h in range(H):
-                    weights, sums = exponentials(edges, neg_shift, h)
-                    if waiting is not None:
-                        finish_head(*waiting)
-                    if h == 0 and first_plane == 0:
-                        attn_sum = keep.tile([P, PACK, N], F32, tag="attn_sum")
-                    waiting = (attn_sum, panel, weights, sums, h)
-                    if panel + 1 < PANELS and h % (H // CHUNKS) == 0:
-                        next_edges.append(prepare_edges(panel + 1, len(next_edges), chunk_top))
-                edges = next_edges
-            finish_head(*waiting)
+        st = new_panel(0)
+        for chunk in range(CHUNKS):
+            load_edges(st, chunk)
+            scale_dist(st, chunk)
+            make_mask(st, chunk)
+            add_bond(st, chunk)
+            make_shared(st, chunk)
+            reduce_shared(st, chunk)
+        panel_tops(st)
+        column_tops(st)
+        negate_scores(st)
+        softmax_shifts(st)
 
-        with tc.tile_pool(name="finish", bufs=2, reuse_waits="tile") as finish:
-            def out_pass(out_ps, it, g):
-                rows = slice(it * P, (it + 1) * P)
+        with tc.tile_pool(name="vwork", bufs=2) as vwork:
+            wv_codes, wv_scales = quantise_wv(vwork)
+            for g in range(PASSES):
+                nf_sb = load_nodes(vwork, g)
+                run_head(st, g)
+                make_v(vwork, g, nf_sb, wv_codes, wv_scales)
+
+        late = ctx.enter_context(tc.tile_pool(name="late", bufs=2, reuse_waits="tile"))
+        attn_codes = late.tile([P, PASSES, N], U32, bufs=1, align_bytes=64)
+        attn_scales = late.tile([P, N], U8, bufs=1, align_bytes=64)
+        for h in range(PASSES, H):
+            run_head(st, h)
+        for panel in range(1, PANELS):
+            st = state["next"]
+            for h in range(H):
+                run_head(st, h)
+        for slot in range(state["slot"], max(schedule) + 1):
+            run_slot()
+
+        for it in range(ROW_TILES):
+            rows = slice(it * P, (it + 1) * P)
+            out_ps = psum.tile([P, F_OUT], F32, tag="bank", name="out_ps")
+            for g in range(PASSES):
                 nc.tensor.matmul_mx(
                     out=out_ps[:],
                     lhsT=attn_codes[:, g, rows].bitcast(FP8X4),
-                    lhsT_scale=attn_scales[:, g, rows],
+                    lhsT_scale=attn_scales[PACK * g :, rows],
                     rhs=v_codes[:, g, :].bitcast(FP8X4),
                     rhs_scale=v_scales[:, g, :],
                     start=(g == 0),
                     stop=(g == PASSES - 1),
                 )
-
-            early = {}
-            for it in range(PSUM_BANKS):
-                early[it] = psum.tile([P, F_OUT], F32, tag="bank", name="out_ps")
-                for g in range(PASSES - 1):
-                    out_pass(early[it], it, g)
-            for it in range(ROW_TILES):
-                if it in early:
-                    out_ps = early[it]
-                else:
-                    out_ps = psum.tile([P, F_OUT], F32, tag="bank", name="out_ps")
-                    for g in range(PASSES - 1):
-                        out_pass(out_ps, it, g)
-                out_pass(out_ps, it, PASSES - 1)
-                exp_t = finish.tile([P, F_OUT], F32)
-                nc.scalar.activation(out=exp_t[:], in_=out_ps[:], func=ACT.Exp)
-                line_t = finish.tile([P, F_OUT], F32)
+            elu_t = work.tile([P, 2, F_OUT], F32, tag="w", bufs=6, name="elu_t")
+            nc.scalar.activation(out=elu_t[:, 0, :], in_=out_ps[:], func=ACT.Exp)
+            if it % 2 == 0:
+                nc.scalar.activation(out=elu_t[:, 1, :], in_=out_ps[:], func=ACT.Relu)
                 nc.vector.tensor_scalar(
-                    out=line_t[:], in0=out_ps[:], scalar1=0.0, scalar2=-1.0, op0=ALU.max, op1=ALU.add
+                    out=elu_t[:, 0, :], in0=elu_t[:, 0, :], scalar1=1.0, scalar2=-1.0, op0=ALU.min, op1=ALU.add
                 )
-                result = finish.tile([P, F_OUT], F32)
-                nc.vector.scalar_tensor_tensor(
-                    out=result[:], in0=exp_t[:], scalar=1.0, in1=line_t[:], op0=ALU.min, op1=ALU.add
-                )
-                nc.sync.dma_start(out=out_rows[:, it, :], in_=result[:])
+                nc.vector.tensor_tensor(out=elu_t[:, 0, :], in0=elu_t[:, 0, :], in1=elu_t[:, 1, :], op=ALU.add)
+                nc.sync.dma_start(out=out_rows[:, it, :], in_=elu_t[:, 0, :])
+                continue
+            nc.vector.tensor_scalar(
+                out=elu_t[:, 1, :], in0=out_ps[:], scalar1=0.0, scalar2=-1.0, op0=ALU.max, op1=ALU.add
+            )
+            nc.vector.scalar_tensor_tensor(
+                out=elu_t[:, 0, :], in0=elu_t[:, 0, :], scalar=1.0, in1=elu_t[:, 1, :], op0=ALU.min, op1=ALU.add
+            )
+            nc.sync.dma_start(out=out_rows[:, it, :], in_=elu_t[:, 0, :])

@@ -34,7 +34,8 @@ PASSES = N // K_PASS
 JT = 2
 PANEL = JT * P
 PANELS = N // PANEL
-LAG = 3
+LAG = 4
+LEAD = 2
 BASE = 0
 
 FLOPS = 2 * N * F_IN * F_OUT + 2 * N * N * F_OUT
@@ -110,6 +111,9 @@ def tile_egatlayer_pa_kernel(
         a_over_rise = const.tile([P, ROW_TILES * H], F32)
         nc.vector.tensor_scalar_mul(out=a_over_rise[:], in0=d_flat, scalar1=1.0 / (RISE * math.sqrt(H)))
 
+        a_part = const.tile([P, ROW_TILES * H], F32)
+        nc.vector.tensor_scalar_mul(out=a_part[:], in0=d_flat, scalar1=SLOPE / (RISE * math.sqrt(H)))
+
         a_t_ps = psum.tile([P, BANK], F32, tag="bank")
         nc.tensor.transpose(out=a_t_ps[:, :P], in_=a_sb[:], identity=ident_f[:])
         a_tile_top = const.tile([P, 1], F32)
@@ -135,6 +139,8 @@ def tile_egatlayer_pa_kernel(
         v_codes = keep.tile([P, PASSES, F_OUT], U32, align_bytes=64)
         v_scales = keep.tile([P, PASSES, F_OUT], U8, align_bytes=64)
 
+        attn_sum = keep.tile([P, PACK, N], F32)
+
         def new_panel(panel):
             return {
                 "panel": panel,
@@ -142,6 +148,7 @@ def tile_egatlayer_pa_kernel(
                 "e": [],
                 "shared": [],
                 "loads": [],
+                "parts": [],
             }
 
         def load_edges(st, chunk):
@@ -235,31 +242,33 @@ def tile_egatlayer_pa_kernel(
                 out=st["neg_shift"][:], in0=st["neg_x"][:], scalar=SLOPE, in1=st["neg_x"][:], op0=ALU.mult, op1=ALU.min
             )
 
+        def load_wv(vwork):
+            vs["wv_sb"] = vwork.tile([P, PACK, F_OUT], BF16, bufs=1, name="wv_sb")
+            nc.sync.dma_start(out=vs["wv_sb"][:].rearrange("p (u e) f -> p u (e f)", u=PAIR), in_=wv_rows)
+
+        def group_wv(vwork):
+            vs["wv_grouped"] = vwork.tile([P, F_OUT, PACK], BF16, bufs=1, align_bytes=64, name="wv_grouped")
+            nc.vector.tensor_copy(out=vs["wv_grouped"][:], in_=vs["wv_sb"][:].rearrange("p t f -> p f t"))
+
         def quantise_wv(vwork):
-            wv_sb = vwork.tile([P, PACK, F_OUT], BF16, bufs=1)
-            nc.sync.dma_start(out=wv_sb[:].rearrange("p (u e) f -> p u (e f)", u=PAIR), in_=wv_rows)
-            wv_grouped = vwork.tile([P, F_OUT, PACK], BF16, bufs=1, align_bytes=64)
-            nc.vector.tensor_copy(out=wv_grouped[:], in_=wv_sb[:].rearrange("p t f -> p f t"))
-            wv_codes = vwork.tile([P, F_OUT], U32, bufs=1, align_bytes=64)
-            wv_scales = vwork.tile([P, F_OUT], U8, bufs=1, align_bytes=64)
+            vs["wv_codes"] = vwork.tile([P, F_OUT], U32, bufs=1, align_bytes=64, name="wv_codes")
+            vs["wv_scales"] = vwork.tile([P, F_OUT], U8, bufs=1, align_bytes=64, name="wv_scales")
             nc.vector.quantize_mx(
-                out=wv_codes[:].bitcast(FP8X4),
-                scales=wv_scales[:],
-                in_=wv_grouped[:].rearrange("p f t -> p (f t)"),
+                out=vs["wv_codes"][:].bitcast(FP8X4),
+                scales=vs["wv_scales"][:],
+                in_=vs["wv_grouped"][:].rearrange("p f t -> p (f t)"),
             )
-            return wv_codes, wv_scales
 
         def load_nodes(vwork, g):
-            nf_sb = vwork.tile([P, PACK, F_IN], BF16, tag="nf_sb", align_bytes=64)
-            nc.sync.dma_start(out=nf_sb[:], in_=nf_rows[g])
-            return nf_sb
+            vs["nf", g] = vwork.tile([P, PACK, F_IN], BF16, tag="nf_sb", align_bytes=64, name="nf_sb")
+            nc.sync.dma_start(out=vs["nf", g][:], in_=nf_rows[g])
 
-        def make_v(vwork, g, nf_sb, wv_codes, wv_scales):
+        def turn_nodes(vwork, g):
             nf_grouped = vwork.tile([P, PACK, P, PACK], BF16, bufs=1, align_bytes=64)
             for half in range(PAIR):
                 words_ps = psum.tile([P, PAIR, PAIR, P], F32, tag="bank", name="words_ps")
                 for s in range(PAIR):
-                    words = nf_sb[:, PAIR * half + s, :].bitcast(F32)
+                    words = vs["nf", g][:, PAIR * half + s, :].bitcast(F32)
                     for u in range(PAIR):
                         nc.tensor.transpose(
                             out=words_ps[:, s, u, :], in_=words[:, u * P : (u + 1) * P], identity=ident_f[:]
@@ -271,35 +280,62 @@ def tile_egatlayer_pa_kernel(
                     .rearrange("p (t r u) -> p t r u", t=PAIR, u=PAIR),
                     in_=words_ps[:].rearrange("p t u r -> p t r u"),
                 )
-            nf_codes = vwork.tile([P, PACK * P], U32, align_bytes=64)
-            nf_scales = vwork.tile([P, PACK * P], U8, align_bytes=64)
+            vs["nf_grouped", g] = nf_grouped
+
+        def quantise_nodes(vwork, g):
+            nf_codes = vwork.tile([P, PACK * P], U32, bufs=1, align_bytes=64)
+            nf_scales = vwork.tile([P, PACK * P], U8, bufs=1, align_bytes=64)
             nc.vector.quantize_mx(
                 out=nf_codes[:].bitcast(FP8X4),
                 scales=nf_scales[:],
-                in_=nf_grouped[:].rearrange("p t r s -> p (t r s)"),
+                in_=vs["nf_grouped", g][:].rearrange("p t r s -> p (t r s)"),
             )
-            v_planes = vwork.tile([P, PACK, F_OUT], BF16)
+            vs["nf_codes", g] = (nf_codes, nf_scales)
+
+        def multiply_nodes(vwork, g):
+            nf_codes, nf_scales = vs["nf_codes", g]
+            v_planes = vwork.tile([P, PACK, F_OUT], BF16, bufs=1)
             for t in range(PACK):
                 v_ps = psum.tile([P, F_OUT], F32, tag="bank")
                 nc.tensor.matmul_mx(
                     out=v_ps[:],
                     lhsT=nf_codes[:, t * P : (t + 1) * P].bitcast(FP8X4),
                     lhsT_scale=nf_scales[:, t * P : (t + 1) * P],
-                    rhs=wv_codes[:].bitcast(FP8X4),
-                    rhs_scale=wv_scales[:],
+                    rhs=vs["wv_codes"][:].bitcast(FP8X4),
+                    rhs_scale=vs["wv_scales"][:],
                     start=True,
                     stop=True,
                 )
                 nc.scalar.activation(
                     out=v_planes[:, t, :], in_=v_ps[:], func=ACT.Copy, scale=1.0 / math.sqrt(F_IN)
                 )
-            v_grouped = vwork.tile([P, F_OUT, PACK], BF16, align_bytes=64)
-            nc.vector.tensor_copy(out=v_grouped[:], in_=v_planes[:].rearrange("p t f -> p f t"))
+            vs["v_planes", g] = v_planes
+
+        def group_v(vwork, g):
+            vs["v_grouped", g] = vwork.tile([P, F_OUT, PACK], BF16, align_bytes=64, name="v_grouped")
+            nc.vector.tensor_copy(out=vs["v_grouped", g][:], in_=vs["v_planes", g][:].rearrange("p t f -> p f t"))
+
+        def quantise_v(vwork, g):
             nc.vector.quantize_mx(
                 out=v_codes[:, g, :].bitcast(FP8X4),
                 scales=v_scales[:, g, :],
-                in_=v_grouped[:].rearrange("p f t -> p (f t)"),
+                in_=vs["v_grouped", g][:].rearrange("p f t -> p (f t)"),
             )
+
+        def plan_v(vwork):
+            at(1, lambda: group_wv(vwork))
+            at(3, lambda: quantise_wv(vwork))
+            for g in range(PASSES):
+                first = 4 * g
+                at(first + 1, lambda g=g: turn_nodes(vwork, g))
+                at(first + 4, lambda g=g: quantise_nodes(vwork, g))
+                at(first + 5, lambda g=g: multiply_nodes(vwork, g))
+                at(first + 8, lambda g=g: group_v(vwork, g))
+                at(first + 9, lambda g=g: quantise_v(vwork, g))
+                if g + 2 < PASSES:
+                    at(first + 3, lambda g=g: load_nodes(vwork, g + 2))
+
+        vs = {}
 
         def new_head():
             return {
@@ -307,23 +343,36 @@ def tile_egatlayer_pa_kernel(
                 "sums": small.tile([P, JT, CHUNKS], F32, tag="sums", name="sums"),
             }
 
-        def exponentials(st, head, h, chunk):
+        def scalar_tiles(h, chunk):
+            return () if h == BASE else (2, 3) if chunk < 3 else (3,)
+
+        def make_part(st, h, chunk):
             e_t = st["e"][chunk]
-            shared_t = st["shared"][chunk]
             head_t = work.tile([P, CB * PANEL], F32, tag="head", bufs=4)
             if h == BASE:
-                nc.scalar.activation(out=head_t[:], in_=e_t[:], func=ACT.Relu)
+                nc.vector.tensor_scalar_max(out=head_t[:], in0=e_t[:], scalar1=0.0)
             else:
                 for b in range(CB):
                     col = (chunk * CB + b) * H + h
-                    nc.vector.tensor_scalar(
-                        out=head_t[:, b * PANEL : (b + 1) * PANEL],
-                        in0=e_t[:, b * PANEL : (b + 1) * PANEL],
-                        scalar1=neg_a[:, col : col + 1],
-                        scalar2=a_over_rise[:, col : col + 1],
-                        op0=ALU.max,
-                        op1=ALU.add,
-                    )
+                    cols = slice(b * PANEL, (b + 1) * PANEL)
+                    if b in scalar_tiles(h, chunk):
+                        nc.scalar.activation(
+                            out=head_t[:, cols], in_=e_t[:, cols], func=ACT.Relu, bias=a_sb[:, col : col + 1]
+                        )
+                    else:
+                        nc.vector.tensor_scalar(
+                            out=head_t[:, cols],
+                            in0=e_t[:, cols],
+                            scalar1=neg_a[:, col : col + 1],
+                            scalar2=a_over_rise[:, col : col + 1],
+                            op0=ALU.max,
+                            op1=ALU.add,
+                        )
+            st["parts"].append(head_t)
+
+        def exponentials(st, head, h, chunk):
+            shared_t = st["shared"][chunk]
+            head_t = st["parts"][h * CHUNKS + chunk]
             for jt in range(JT):
                 bank = psum.tile([P, BANK], F32, tag="bank")
                 for b in range(CB):
@@ -334,8 +383,14 @@ def tile_egatlayer_pa_kernel(
                     )
                     nc.tensor.matmul(
                         out=bank[:, b * P : (b + 1) * P], lhsT=shared_t[:, cols], rhs=ident_f[:],
-                        is_transpose=True, start=False, stop=True,
+                        is_transpose=True, start=False, stop=b not in scalar_tiles(h, chunk),
                     )
+                    if b in scalar_tiles(h, chunk):
+                        col = (chunk * CB + b) * H + h
+                        nc.tensor.matmul(
+                            out=bank[:, b * P : (b + 1) * P], lhsT=a_part[:, col : col + 1].to_broadcast([P, P]),
+                            rhs=ident_f[:], is_transpose=True, start=False, stop=True,
+                        )
                 nc.scalar.activation(
                     out=head["w"][jt][:, chunk * BANK : (chunk + 1) * BANK],
                     in_=bank[:],
@@ -354,12 +409,10 @@ def tile_egatlayer_pa_kernel(
             nc.vector.reciprocal(out=head["inverse"][:], in_=head["total"][:])
 
         def add_head(panel, head, h, jt, cols):
-            if h == 0 and jt == 0 and panel % PAIR == 0:
-                state["attn_sum"] = keep.tile([P, PACK, N], F32, tag="attn_sum", name="attn_sum")
-            plane = state["attn_sum"][:, (panel % PAIR) * JT + jt, cols]
+            plane = attn_sum[:, (panel % PAIR) * JT + jt, cols]
             scale = head["inverse"][:, jt : jt + 1]
             if h == 0:
-                nc.scalar.activation(out=plane, in_=head["w"][jt][:, cols], func=ACT.Copy, scale=scale)
+                nc.vector.tensor_scalar_mul(out=plane, in0=head["w"][jt][:, cols], scalar1=scale)
             else:
                 nc.vector.scalar_tensor_tensor(
                     out=plane, in0=head["w"][jt][:, cols], scalar=scale, in1=plane, op0=ALU.mult, op1=ALU.add
@@ -367,25 +420,22 @@ def tile_egatlayer_pa_kernel(
 
         def group_mean(g, chunk):
             cols = slice(chunk * BANK, (chunk + 1) * BANK)
-            grouped = late.tile([P, BANK, PACK], BF16, tag="grouped", align_bytes=64, name="grouped")
+            grouped = late.tile([P, BANK, PACK], BF16, tag="grouped", bufs=3, align_bytes=64, name="grouped")
             nc.scalar.activation(
                 out=grouped[:],
-                in_=state["attn_sum"][:, :, cols].rearrange("p t i -> p i t"),
+                in_=attn_sum[:, :, cols].rearrange("p t i -> p i t"),
                 func=ACT.Copy,
                 scale=1.0 / H,
             )
-            return grouped
+            state["grouped", g, chunk] = grouped
 
-        def quantise_mean(g, chunk, grouped):
+        def quantise_mean(g, chunk):
             cols = slice(chunk * BANK, (chunk + 1) * BANK)
             nc.vector.quantize_mx(
                 out=attn_codes[:, g, cols].bitcast(FP8X4),
                 scales=attn_scales[PACK * g :, cols],
-                in_=grouped[:].rearrange("p i t -> p (i t)"),
+                in_=state["grouped", g, chunk][:].rearrange("p i t -> p (i t)"),
             )
-
-        def mean_step(g, chunk):
-            quantise_mean(g, chunk, group_mean(g, chunk))
 
         state = {"slot": 0}
         schedule = {}
@@ -401,30 +451,30 @@ def tile_egatlayer_pa_kernel(
         def plan_head(panel, head, h, slot):
             at(slot + LAG, lambda: add_sums(head))
             at(slot + LAG + 1, lambda: invert_sums(head))
-            if panel == PANELS - 1 and h == H - 1:
-                for chunk in range(CHUNKS):
-                    for jt in range(JT):
-                        at(slot + LAG + 2, lambda jt=jt, chunk=chunk: add_head(panel, head, h, jt, slice(chunk * BANK, (chunk + 1) * BANK)))
-                    at(slot + LAG + 2, lambda chunk=chunk: mean_step(panel // PAIR, chunk))
-            else:
+            last = h == H - 1 and panel % PAIR == PAIR - 1
+            g = panel // PAIR
+            late_by = 2 if h == 0 and panel % PAIR == 0 else 0
+            for half in range(2):
                 for jt in range(JT):
-                    at(slot + LAG + 2 + jt, lambda jt=jt: add_head(panel, head, h, jt, slice(0, N)))
-                if h == H - 1 and panel % PAIR == PAIR - 1:
-                    for chunk in range(CHUNKS):
-                        at(slot + LAG + 4 + chunk // 2, lambda chunk=chunk: mean_step(panel // PAIR, chunk))
+                    cols = slice(half * N // 2, (half + 1) * N // 2)
+                    at(slot + LAG + 2 + 2 * half + jt + late_by, lambda jt=jt, cols=cols: add_head(panel, head, h, jt, cols))
+                if last:
+                    for chunk in (2 * half, 2 * half + 1):
+                        at(slot + LAG + 4 + chunk, lambda chunk=chunk: group_mean(g, chunk))
+                        at(slot + LAG + 4 + chunk + 4, lambda chunk=chunk: quantise_mean(g, chunk))
 
         def plan_edges(st, slot):
             for chunk in range(CHUNKS):
-                first = slot + 7 * chunk
+                first = slot + 6 * chunk
                 at(first, lambda chunk=chunk: load_edges(st, chunk))
-                at(first + 2, lambda chunk=chunk: scale_dist(st, chunk))
-                at(first + 2, lambda chunk=chunk: make_mask(st, chunk))
-                at(first + 3, lambda chunk=chunk: add_bond(st, chunk))
-                at(first + 4, lambda chunk=chunk: make_shared(st, chunk))
-                at(first + 5, lambda chunk=chunk: reduce_shared(st, chunk))
+                at(first + 1, lambda chunk=chunk: scale_dist(st, chunk))
+                at(first + 5, lambda chunk=chunk: make_mask(st, chunk))
+                at(first + 6, lambda chunk=chunk: add_bond(st, chunk))
+                at(first + 7, lambda chunk=chunk: make_shared(st, chunk))
+                at(first + 8, lambda chunk=chunk: reduce_shared(st, chunk))
             at(slot + 27, lambda: panel_tops(st))
-            at(slot + 29, lambda: column_tops(st))
-            at(slot + 30, lambda: negate_scores(st))
+            at(slot + 30, lambda: column_tops(st))
+            at(slot + 31, lambda: negate_scores(st))
             at(slot + 31, lambda: softmax_shifts(st))
 
         def run_head(st, h):
@@ -433,6 +483,11 @@ def tile_egatlayer_pa_kernel(
                 plan_edges(state["next"], state["slot"])
             head = new_head()
             for chunk in range(CHUNKS):
+                ahead = h * CHUNKS + chunk + LEAD
+                if ahead < H * CHUNKS:
+                    make_part(st, ahead // CHUNKS, ahead % CHUNKS)
+                elif "next" in state and state["next"]["panel"] > st["panel"]:
+                    make_part(state["next"], 0, ahead - H * CHUNKS)
                 exponentials(st, head, h, chunk)
                 run_slot()
             plan_head(st["panel"], head, h, state["slot"])
@@ -449,23 +504,27 @@ def tile_egatlayer_pa_kernel(
         column_tops(st)
         negate_scores(st)
         softmax_shifts(st)
+        for chunk in range(LEAD):
+            make_part(st, 0, chunk)
 
-        with tc.tile_pool(name="vwork", bufs=2) as vwork:
-            wv_codes, wv_scales = quantise_wv(vwork)
-            for g in range(PASSES):
-                nf_sb = load_nodes(vwork, g)
-                run_head(st, g)
-                make_v(vwork, g, nf_sb, wv_codes, wv_scales)
+        with tc.manual_schedule(engines={mybir.EngineType.DVE, mybir.EngineType.Activation, mybir.EngineType.PE}):
+            with tc.tile_pool(name="vwork", bufs=2) as vwork:
+                load_wv(vwork)
+                load_nodes(vwork, 0)
+                load_nodes(vwork, 1)
+                plan_v(vwork)
+                for h in range(6):
+                    run_head(st, h)
 
-        late = ctx.enter_context(tc.tile_pool(name="late", bufs=2, reuse_waits="tile"))
-        attn_codes = late.tile([P, PASSES, N], U32, bufs=1, align_bytes=64)
-        attn_scales = late.tile([P, N], U8, bufs=1, align_bytes=64)
-        for h in range(PASSES, H):
-            run_head(st, h)
-        for panel in range(1, PANELS):
-            st = state["next"]
-            for h in range(H):
+            late = ctx.enter_context(tc.tile_pool(name="late", bufs=2, reuse_waits="tile"))
+            attn_codes = late.tile([P, PASSES, N], U32, bufs=1, align_bytes=64)
+            attn_scales = late.tile([P, N], U8, bufs=1, align_bytes=64)
+            for h in range(6, H):
                 run_head(st, h)
+            for panel in range(1, PANELS):
+                st = state["next"]
+                for h in range(H):
+                    run_head(st, h)
         for slot in range(state["slot"], max(schedule) + 1):
             run_slot()
 

@@ -34,8 +34,8 @@ PASSES = N // K_PASS
 JT = 2
 PANEL = JT * P
 PANELS = N // PANEL
-LAG = 4
-LEAD = 2
+LAG = 3
+LEAD = 4
 BASE = 0
 
 FLOPS = 2 * N * F_IN * F_OUT + 2 * N * N * F_OUT
@@ -144,7 +144,8 @@ def tile_egatlayer_pa_kernel(
         def new_panel(panel):
             return {
                 "panel": panel,
-                "top": stage.tile([P, CHUNKS, PANEL], F32, tag="chunk_top", bufs=1, name="chunk_top"),
+                "top": stage.tile([P, PANEL], F32, tag="panel_top", name="panel_top"),
+                "chunk_top": {},
                 "e": [],
                 "shared": [],
                 "loads": [],
@@ -196,23 +197,26 @@ def tile_egatlayer_pa_kernel(
             st["shared"].append(shared_t)
 
         def reduce_shared(st, chunk):
+            chunk_top = st["top"]
+            if chunk > 0:
+                chunk_top = stage.tile([P, PANEL], F32, tag="chunk_top", name="chunk_top")
             nc.vector.tensor_reduce(
-                out=st["top"][:, chunk, :],
+                out=chunk_top[:],
                 in_=st["shared"][chunk][:].rearrange("p (b j) -> p j b", b=CB),
                 axis=AX.X,
                 op=ALU.max,
             )
+            st["chunk_top"][chunk] = chunk_top
 
-        def panel_tops(st):
-            panel_top = stage.tile([P, PANEL], F32, tag="panel_top", bufs=1)
-            nc.vector.tensor_reduce(
-                out=panel_top[:], in_=st["top"][:].rearrange("p c j -> p j c"), axis=AX.X, op=ALU.max
-            )
+        def join_tops(st, chunk):
+            nc.vector.tensor_tensor(out=st["top"][:], in0=st["top"][:], in1=st["chunk_top"][chunk][:], op=ALU.max)
+
+        def turn_tops(st):
             st["top_bank"] = psum.tile([P, BANK], F32, tag="bank", name="top_bank")
             for jt in range(JT):
                 nc.tensor.transpose(
                     out=st["top_bank"][:, jt * P : (jt + 1) * P],
-                    in_=panel_top[:, jt * P : (jt + 1) * P],
+                    in_=st["top"][:, jt * P : (jt + 1) * P],
                     identity=ident_f[:],
                 )
 
@@ -312,7 +316,7 @@ def tile_egatlayer_pa_kernel(
             vs["v_planes", g] = v_planes
 
         def group_v(vwork, g):
-            vs["v_grouped", g] = vwork.tile([P, F_OUT, PACK], BF16, align_bytes=64, name="v_grouped")
+            vs["v_grouped", g] = vwork.tile([P, F_OUT, PACK], BF16, bufs=1, align_bytes=64, name="v_grouped")
             nc.vector.tensor_copy(out=vs["v_grouped", g][:], in_=vs["v_planes", g][:].rearrange("p t f -> p f t"))
 
         def quantise_v(vwork, g):
@@ -343,19 +347,23 @@ def tile_egatlayer_pa_kernel(
                 "sums": small.tile([P, JT, CHUNKS], F32, tag="sums", name="sums"),
             }
 
-        def scalar_tiles(h, chunk):
-            return () if h == BASE else (2, 3) if chunk < 3 else (3,)
+        def scalar_tiles(panel, h, chunk):
+            if h == BASE:
+                return ()
+            if panel == PANELS - 1:
+                return (3,)
+            return (2, 3) if chunk < 3 else (3,)
 
         def make_part(st, h, chunk):
             e_t = st["e"][chunk]
-            head_t = work.tile([P, CB * PANEL], F32, tag="head", bufs=4)
+            head_t = work.tile([P, CB * PANEL], F32, tag="head", bufs=7, align_bytes=64, name="head_t")
             if h == BASE:
                 nc.vector.tensor_scalar_max(out=head_t[:], in0=e_t[:], scalar1=0.0)
             else:
                 for b in range(CB):
                     col = (chunk * CB + b) * H + h
                     cols = slice(b * PANEL, (b + 1) * PANEL)
-                    if b in scalar_tiles(h, chunk):
+                    if b in scalar_tiles(st["panel"], h, chunk):
                         nc.scalar.activation(
                             out=head_t[:, cols], in_=e_t[:, cols], func=ACT.Relu, bias=a_sb[:, col : col + 1]
                         )
@@ -383,9 +391,9 @@ def tile_egatlayer_pa_kernel(
                     )
                     nc.tensor.matmul(
                         out=bank[:, b * P : (b + 1) * P], lhsT=shared_t[:, cols], rhs=ident_f[:],
-                        is_transpose=True, start=False, stop=b not in scalar_tiles(h, chunk),
+                        is_transpose=True, start=False, stop=b not in scalar_tiles(st["panel"], h, chunk),
                     )
-                    if b in scalar_tiles(h, chunk):
+                    if b in scalar_tiles(st["panel"], h, chunk):
                         col = (chunk * CB + b) * H + h
                         nc.tensor.matmul(
                             out=bank[:, b * P : (b + 1) * P], lhsT=a_part[:, col : col + 1].to_broadcast([P, P]),
@@ -418,15 +426,14 @@ def tile_egatlayer_pa_kernel(
                     out=plane, in0=head["w"][jt][:, cols], scalar=scale, in1=plane, op0=ALU.mult, op1=ALU.add
                 )
 
-        def group_mean(g, chunk):
+        def group_mean(g, chunk, on_vector=False):
             cols = slice(chunk * BANK, (chunk + 1) * BANK)
-            grouped = late.tile([P, BANK, PACK], BF16, tag="grouped", bufs=3, align_bytes=64, name="grouped")
-            nc.scalar.activation(
-                out=grouped[:],
-                in_=attn_sum[:, :, cols].rearrange("p t i -> p i t"),
-                func=ACT.Copy,
-                scale=1.0 / H,
-            )
+            grouped = work.tile([P, BANK, PACK], BF16, tag="head", bufs=7, align_bytes=64, name="grouped")
+            planes = attn_sum[:, :, cols].rearrange("p t i -> p i t")
+            if on_vector:
+                nc.vector.tensor_scalar_mul(out=grouped[:], in0=planes, scalar1=1.0 / H)
+            else:
+                nc.scalar.activation(out=grouped[:], in_=planes, func=ACT.Copy, scale=1.0 / H)
             state["grouped", g, chunk] = grouped
 
         def quantise_mean(g, chunk):
@@ -449,19 +456,26 @@ def tile_egatlayer_pa_kernel(
             state["slot"] = state["slot"] + 1
 
         def plan_head(panel, head, h, slot):
-            at(slot + LAG, lambda: add_sums(head))
-            at(slot + LAG + 1, lambda: invert_sums(head))
+            if panel == PANELS - 1 and h == H - 1:
+                return
+            lag = LAG
+            if panel == PANELS - 1 and h == H - 2:
+                lag = 1
+            at(slot + lag, lambda: add_sums(head))
+            at(slot + lag + 1, lambda: invert_sums(head))
             last = h == H - 1 and panel % PAIR == PAIR - 1
             g = panel // PAIR
-            late_by = 2 if h == 0 and panel % PAIR == 0 else 0
+            first = slot + lag + 2
+            if h == 0 and panel % PAIR == 0:
+                first = first + 2
             for half in range(2):
                 for jt in range(JT):
                     cols = slice(half * N // 2, (half + 1) * N // 2)
-                    at(slot + LAG + 2 + 2 * half + jt + late_by, lambda jt=jt, cols=cols: add_head(panel, head, h, jt, cols))
+                    at(min(first + 2 * half + jt, PANELS * H * CHUNKS - 1), lambda jt=jt, cols=cols: add_head(panel, head, h, jt, cols))
                 if last:
                     for chunk in (2 * half, 2 * half + 1):
-                        at(slot + LAG + 4 + chunk, lambda chunk=chunk: group_mean(g, chunk))
-                        at(slot + LAG + 4 + chunk + 4, lambda chunk=chunk: quantise_mean(g, chunk))
+                        at(first + 2 + chunk, lambda chunk=chunk: group_mean(g, chunk))
+                        at(first + 2 + chunk + 4, lambda chunk=chunk: quantise_mean(g, chunk))
 
         def plan_edges(st, slot):
             for chunk in range(CHUNKS):
@@ -472,7 +486,9 @@ def tile_egatlayer_pa_kernel(
                 at(first + 6, lambda chunk=chunk: add_bond(st, chunk))
                 at(first + 7, lambda chunk=chunk: make_shared(st, chunk))
                 at(first + 8, lambda chunk=chunk: reduce_shared(st, chunk))
-            at(slot + 27, lambda: panel_tops(st))
+                if chunk > 0:
+                    at(first + 9, lambda chunk=chunk: join_tops(st, chunk))
+            at(slot + 28, lambda: turn_tops(st))
             at(slot + 30, lambda: column_tops(st))
             at(slot + 31, lambda: negate_scores(st))
             at(slot + 31, lambda: softmax_shifts(st))
@@ -491,6 +507,7 @@ def tile_egatlayer_pa_kernel(
                 exponentials(st, head, h, chunk)
                 run_slot()
             plan_head(st["panel"], head, h, state["slot"])
+            return head
 
         st = new_panel(0)
         for chunk in range(CHUNKS):
@@ -500,7 +517,9 @@ def tile_egatlayer_pa_kernel(
             add_bond(st, chunk)
             make_shared(st, chunk)
             reduce_shared(st, chunk)
-        panel_tops(st)
+            if chunk > 0:
+                join_tops(st, chunk)
+        turn_tops(st)
         column_tops(st)
         negate_scores(st)
         softmax_shifts(st)
@@ -524,23 +543,20 @@ def tile_egatlayer_pa_kernel(
             for panel in range(1, PANELS):
                 st = state["next"]
                 for h in range(H):
-                    run_head(st, h)
-        for slot in range(state["slot"], max(schedule) + 1):
-            run_slot()
-
-        for it in range(ROW_TILES):
+                    head = run_head(st, h)
+        def out_pass(out_ps, it, g):
             rows = slice(it * P, (it + 1) * P)
-            out_ps = psum.tile([P, F_OUT], F32, tag="bank", name="out_ps")
-            for g in range(PASSES):
-                nc.tensor.matmul_mx(
-                    out=out_ps[:],
-                    lhsT=attn_codes[:, g, rows].bitcast(FP8X4),
-                    lhsT_scale=attn_scales[PACK * g :, rows],
-                    rhs=v_codes[:, g, :].bitcast(FP8X4),
-                    rhs_scale=v_scales[:, g, :],
-                    start=(g == 0),
-                    stop=(g == PASSES - 1),
-                )
+            nc.tensor.matmul_mx(
+                out=out_ps[:],
+                lhsT=attn_codes[:, g, rows].bitcast(FP8X4),
+                lhsT_scale=attn_scales[PACK * g :, rows],
+                rhs=v_codes[:, g, :].bitcast(FP8X4),
+                rhs_scale=v_scales[:, g, :],
+                start=(g == 0),
+                stop=(g == PASSES - 1),
+            )
+
+        def finish_rows(out_ps, it):
             elu_t = work.tile([P, 2, F_OUT], F32, tag="w", bufs=6, name="elu_t")
             nc.scalar.activation(out=elu_t[:, 0, :], in_=out_ps[:], func=ACT.Exp)
             if it % 2 == 0:
@@ -549,12 +565,34 @@ def tile_egatlayer_pa_kernel(
                     out=elu_t[:, 0, :], in0=elu_t[:, 0, :], scalar1=1.0, scalar2=-1.0, op0=ALU.min, op1=ALU.add
                 )
                 nc.vector.tensor_tensor(out=elu_t[:, 0, :], in0=elu_t[:, 0, :], in1=elu_t[:, 1, :], op=ALU.add)
-                nc.sync.dma_start(out=out_rows[:, it, :], in_=elu_t[:, 0, :])
-                continue
-            nc.vector.tensor_scalar(
-                out=elu_t[:, 1, :], in0=out_ps[:], scalar1=0.0, scalar2=-1.0, op0=ALU.max, op1=ALU.add
-            )
-            nc.vector.scalar_tensor_tensor(
-                out=elu_t[:, 0, :], in0=elu_t[:, 0, :], scalar=1.0, in1=elu_t[:, 1, :], op0=ALU.min, op1=ALU.add
-            )
+            else:
+                nc.vector.tensor_scalar(
+                    out=elu_t[:, 1, :], in0=out_ps[:], scalar1=0.0, scalar2=-1.0, op0=ALU.max, op1=ALU.add
+                )
+                nc.vector.scalar_tensor_tensor(
+                    out=elu_t[:, 0, :], in0=elu_t[:, 0, :], scalar=1.0, in1=elu_t[:, 1, :], op0=ALU.min, op1=ALU.add
+                )
             nc.sync.dma_start(out=out_rows[:, it, :], in_=elu_t[:, 0, :])
+
+        add_sums(head)
+        invert_sums(head)
+        for chunk in range(CHUNKS):
+            for jt in range(JT):
+                add_head(PANELS - 1, head, H - 1, jt, slice(chunk * BANK, (chunk + 1) * BANK))
+            group_mean(PASSES - 1, chunk, on_vector=chunk == CHUNKS - 1)
+        early = []
+        for it in range(8):
+            early.append(psum.tile([P, F_OUT], F32, tag="bank", name="out_ps"))
+            for g in range(PASSES - 1):
+                out_pass(early[it], it, g)
+        for chunk in range(CHUNKS):
+            quantise_mean(PASSES - 1, chunk)
+            for it in range(chunk * CB, (chunk + 1) * CB):
+                if it < 8:
+                    out_ps = early[it]
+                else:
+                    out_ps = psum.tile([P, F_OUT], F32, tag="bank", name="out_ps")
+                    for g in range(PASSES - 1):
+                        out_pass(out_ps, it, g)
+                out_pass(out_ps, it, PASSES - 1)
+                finish_rows(out_ps, it)

@@ -34,7 +34,12 @@ PASSES = N // K_PASS
 JT = 2
 PANEL = JT * P
 PANELS = N // PANEL
-LAG = 3
+LAG = 1
+SPREAD = 3
+VS = 4
+JOIN = 20
+TURN = 24
+COL = 26
 LEAD = 4
 BASE = 0
 
@@ -144,8 +149,7 @@ def tile_egatlayer_pa_kernel(
         def new_panel(panel):
             return {
                 "panel": panel,
-                "top": stage.tile([P, PANEL], F32, tag="panel_top", name="panel_top"),
-                "chunk_top": {},
+                "top": stage.tile([P, PAIR * PANEL], F32, tag="panel_top", name="panel_top"),
                 "e": [],
                 "shared": [],
                 "loads": [],
@@ -196,20 +200,23 @@ def tile_egatlayer_pa_kernel(
             )
             st["shared"].append(shared_t)
 
-        def reduce_shared(st, chunk):
-            chunk_top = st["top"]
+        def raise_tops(st, chunk):
+            shared_t = st["shared"][chunk]
+            pairs = [shared_t[:, n * PAIR * PANEL : (n + 1) * PAIR * PANEL] for n in range(CB // PAIR)]
             if chunk > 0:
-                chunk_top = stage.tile([P, PANEL], F32, tag="chunk_top", name="chunk_top")
-            nc.vector.tensor_reduce(
-                out=chunk_top[:],
-                in_=st["shared"][chunk][:].rearrange("p (b j) -> p j b", b=CB),
-                axis=AX.X,
-                op=ALU.max,
-            )
-            st["chunk_top"][chunk] = chunk_top
+                pairs.append(st["top"][:])
+            nc.vector.tensor_tensor(out=st["top"][:], in0=pairs[0], in1=pairs[-1], op=ALU.max)
 
-        def join_tops(st, chunk):
-            nc.vector.tensor_tensor(out=st["top"][:], in0=st["top"][:], in1=st["chunk_top"][chunk][:], op=ALU.max)
+        def raise_tops_again(st, chunk):
+            shared_t = st["shared"][chunk]
+            nc.vector.tensor_tensor(
+                out=st["top"][:], in0=shared_t[:, PAIR * PANEL :], in1=st["top"][:], op=ALU.max
+            )
+
+        def join_tops(st):
+            nc.vector.tensor_tensor(
+                out=st["top"][:, :PANEL], in0=st["top"][:, :PANEL], in1=st["top"][:, PANEL:], op=ALU.max
+            )
 
         def turn_tops(st):
             st["top_bank"] = psum.tile([P, BANK], F32, tag="bank", name="top_bank")
@@ -458,16 +465,13 @@ def tile_egatlayer_pa_kernel(
         def plan_head(panel, head, h, slot):
             if panel == PANELS - 1 and h == H - 1:
                 return
-            lag = LAG
-            if panel == PANELS - 1 and h == H - 2:
-                lag = 1
-            at(slot + lag, lambda: add_sums(head))
-            at(slot + lag + 1, lambda: invert_sums(head))
+            at(slot + LAG, lambda: add_sums(head))
+            at(slot + LAG + 1, lambda: invert_sums(head))
             last = h == H - 1 and panel % PAIR == PAIR - 1
             g = panel // PAIR
-            first = slot + lag + 2
+            first = slot + LAG + 2
             if h == 0 and panel % PAIR == 0:
-                first = first + 2
+                first = first + 3
             for half in range(2):
                 for jt in range(JT):
                     cols = slice(half * N // 2, (half + 1) * N // 2)
@@ -479,19 +483,20 @@ def tile_egatlayer_pa_kernel(
 
         def plan_edges(st, slot):
             for chunk in range(CHUNKS):
-                first = slot + 6 * chunk
-                at(first, lambda chunk=chunk: load_edges(st, chunk))
+                first = slot + SPREAD * chunk
+                at(first + 0, lambda chunk=chunk: load_edges(st, chunk))
                 at(first + 1, lambda chunk=chunk: scale_dist(st, chunk))
-                at(first + 5, lambda chunk=chunk: make_mask(st, chunk))
-                at(first + 6, lambda chunk=chunk: add_bond(st, chunk))
-                at(first + 7, lambda chunk=chunk: make_shared(st, chunk))
-                at(first + 8, lambda chunk=chunk: reduce_shared(st, chunk))
+                at(first + VS, lambda chunk=chunk: make_mask(st, chunk))
+                at(first + VS + 1, lambda chunk=chunk: add_bond(st, chunk))
+                at(first + VS + 2, lambda chunk=chunk: make_shared(st, chunk))
+                at(first + VS + 3, lambda chunk=chunk: raise_tops(st, chunk))
                 if chunk > 0:
-                    at(first + 9, lambda chunk=chunk: join_tops(st, chunk))
-            at(slot + 28, lambda: turn_tops(st))
-            at(slot + 30, lambda: column_tops(st))
-            at(slot + 31, lambda: negate_scores(st))
-            at(slot + 31, lambda: softmax_shifts(st))
+                    at(first + VS + 4, lambda chunk=chunk: raise_tops_again(st, chunk))
+            at(slot + JOIN, lambda: join_tops(st))
+            at(slot + TURN, lambda: turn_tops(st))
+            at(slot + COL, lambda: column_tops(st))
+            at(slot + COL + 1, lambda: negate_scores(st))
+            at(slot + COL + 1, lambda: softmax_shifts(st))
 
         def run_head(st, h):
             if h == 0 and st["panel"] + 1 < PANELS:
@@ -516,9 +521,10 @@ def tile_egatlayer_pa_kernel(
             make_mask(st, chunk)
             add_bond(st, chunk)
             make_shared(st, chunk)
-            reduce_shared(st, chunk)
+            raise_tops(st, chunk)
             if chunk > 0:
-                join_tops(st, chunk)
+                raise_tops_again(st, chunk)
+        join_tops(st)
         turn_tops(st)
         column_tops(st)
         negate_scores(st)
@@ -559,7 +565,7 @@ def tile_egatlayer_pa_kernel(
         def finish_rows(out_ps, it):
             elu_t = work.tile([P, 2, F_OUT], F32, tag="w", bufs=6, name="elu_t")
             nc.scalar.activation(out=elu_t[:, 0, :], in_=out_ps[:], func=ACT.Exp)
-            if it % 2 == 0:
+            if it % 4 != 3:
                 nc.scalar.activation(out=elu_t[:, 1, :], in_=out_ps[:], func=ACT.Relu)
                 nc.vector.tensor_scalar(
                     out=elu_t[:, 0, :], in0=elu_t[:, 0, :], scalar1=1.0, scalar2=-1.0, op0=ALU.min, op1=ALU.add
@@ -574,25 +580,28 @@ def tile_egatlayer_pa_kernel(
                 )
             nc.sync.dma_start(out=out_rows[:, it, :], in_=elu_t[:, 0, :])
 
-        add_sums(head)
-        invert_sums(head)
-        for chunk in range(CHUNKS):
-            for jt in range(JT):
-                add_head(PANELS - 1, head, H - 1, jt, slice(chunk * BANK, (chunk + 1) * BANK))
-            group_mean(PASSES - 1, chunk, on_vector=chunk == CHUNKS - 1)
-        early = []
-        for it in range(8):
-            early.append(psum.tile([P, F_OUT], F32, tag="bank", name="out_ps"))
-            for g in range(PASSES - 1):
-                out_pass(early[it], it, g)
-        for chunk in range(CHUNKS):
-            quantise_mean(PASSES - 1, chunk)
-            for it in range(chunk * CB, (chunk + 1) * CB):
-                if it < 8:
-                    out_ps = early[it]
-                else:
-                    out_ps = psum.tile([P, F_OUT], F32, tag="bank", name="out_ps")
+        with tc.manual_schedule(engines={mybir.EngineType.DVE, mybir.EngineType.Activation, mybir.EngineType.PE}):
+            add_sums(head)
+            invert_sums(head)
+            for chunk in range(CHUNKS):
+                for jt in range(JT):
+                    add_head(PANELS - 1, head, H - 1, jt, slice(chunk * BANK, (chunk + 1) * BANK))
+            banks = []
+            for it in range(8):
+                banks.append(psum.tile([P, F_OUT], F32, tag="bank", name="out_ps"))
+                for g in range(PASSES - 1):
+                    out_pass(banks[it], it, g)
+            for chunk in range(2):
+                group_mean(PASSES - 1, chunk)
+            quantise_mean(PASSES - 1, 0)
+            for chunk in range(2, CHUNKS):
+                group_mean(PASSES - 1, chunk, on_vector=True)
+            for chunk in range(1, CHUNKS):
+                quantise_mean(PASSES - 1, chunk)
+            for it in range(ROW_TILES):
+                if it >= 8:
+                    banks.append(psum.tile([P, F_OUT], F32, tag="bank", name="out_ps"))
                     for g in range(PASSES - 1):
-                        out_pass(out_ps, it, g)
-                out_pass(out_ps, it, PASSES - 1)
-                finish_rows(out_ps, it)
+                        out_pass(banks[it], it, g)
+                out_pass(banks[it], it, PASSES - 1)
+                finish_rows(banks[it], it)

@@ -357,14 +357,16 @@ def tile_egatlayer_pa_kernel(
         def scalar_tiles(panel, h, chunk):
             if h == BASE:
                 return ()
-            if panel == PANELS - 1:
+            if panel in (0, PANELS - 1):
                 return (3,)
             return (2, 3) if chunk < 3 else (3,)
 
         def make_part(st, h, chunk):
             e_t = st["e"][chunk]
             head_t = work.tile([P, CB * PANEL], F32, tag="head", bufs=7, align_bytes=64, name="head_t")
-            if h == BASE:
+            if h == BASE and st["panel"] == 0:
+                nc.scalar.activation(out=head_t[:], in_=e_t[:], func=ACT.Relu)
+            elif h == BASE:
                 nc.vector.tensor_scalar_max(out=head_t[:], in0=e_t[:], scalar1=0.0)
             else:
                 for b in range(CB):
@@ -515,22 +517,26 @@ def tile_egatlayer_pa_kernel(
             return head
 
         st = new_panel(0)
-        for chunk in range(CHUNKS):
-            load_edges(st, chunk)
-            scale_dist(st, chunk)
-            make_mask(st, chunk)
-            add_bond(st, chunk)
-            make_shared(st, chunk)
-            raise_tops(st, chunk)
-            if chunk > 0:
-                raise_tops_again(st, chunk)
-        join_tops(st)
-        turn_tops(st)
-        column_tops(st)
-        negate_scores(st)
-        softmax_shifts(st)
-        for chunk in range(LEAD):
-            make_part(st, 0, chunk)
+        with tc.manual_schedule(engines={mybir.EngineType.DVE, mybir.EngineType.Activation, mybir.EngineType.PE}):
+            for chunk in range(CHUNKS):
+                load_edges(st, chunk)
+                scale_dist(st, chunk)
+                add_bond(st, chunk)
+                make_mask(st, chunk)
+                if chunk > 0:
+                    raise_tops(st, chunk - 1)
+                make_shared(st, chunk)
+                if chunk > 1:
+                    raise_tops_again(st, chunk - 1)
+            for chunk in range(LEAD):
+                make_part(st, 0, chunk)
+            raise_tops(st, CHUNKS - 1)
+            raise_tops_again(st, CHUNKS - 1)
+            join_tops(st)
+            turn_tops(st)
+            column_tops(st)
+            negate_scores(st)
+            softmax_shifts(st)
 
         with tc.manual_schedule(engines={mybir.EngineType.DVE, mybir.EngineType.Activation, mybir.EngineType.PE}):
             with tc.tile_pool(name="vwork", bufs=2) as vwork:

@@ -357,9 +357,9 @@ def tile_egatlayer_pa_kernel(
         def scalar_tiles(panel, h, chunk):
             if h == BASE:
                 return ()
-            if panel in (0, PANELS - 1):
+            if panel == PANELS - 1:
                 return (3,)
-            return (2, 3) if chunk < 3 else (3,)
+            return (1, 2, 3) if chunk == 0 else (2, 3)
 
         def make_part(st, h, chunk):
             e_t = st["e"][chunk]
@@ -395,11 +395,11 @@ def tile_egatlayer_pa_kernel(
                 for b in range(CB):
                     cols = slice(b * PANEL + jt * P, b * PANEL + (jt + 1) * P)
                     nc.tensor.matmul(
-                        out=bank[:, b * P : (b + 1) * P], lhsT=head_t[:, cols], rhs=ident_f[:],
+                        out=bank[:, b * P : (b + 1) * P], lhsT=shared_t[:, cols], rhs=ident_f[:],
                         is_transpose=True, start=True, stop=False,
                     )
                     nc.tensor.matmul(
-                        out=bank[:, b * P : (b + 1) * P], lhsT=shared_t[:, cols], rhs=ident_f[:],
+                        out=bank[:, b * P : (b + 1) * P], lhsT=head_t[:, cols], rhs=ident_f[:],
                         is_transpose=True, start=False, stop=b not in scalar_tiles(st["panel"], h, chunk),
                     )
                     if b in scalar_tiles(st["panel"], h, chunk):
@@ -472,16 +472,14 @@ def tile_egatlayer_pa_kernel(
             last = h == H - 1 and panel % PAIR == PAIR - 1
             g = panel // PAIR
             first = slot + LAG + 2
-            if h == 0 and panel % PAIR == 0:
-                first = first + 3
             for half in range(2):
                 for jt in range(JT):
                     cols = slice(half * N // 2, (half + 1) * N // 2)
                     at(min(first + 2 * half + jt, PANELS * H * CHUNKS - 1), lambda jt=jt, cols=cols: add_head(panel, head, h, jt, cols))
                 if last:
                     for chunk in (2 * half, 2 * half + 1):
-                        at(first + 2 + chunk, lambda chunk=chunk: group_mean(g, chunk))
-                        at(first + 2 + chunk + 4, lambda chunk=chunk: quantise_mean(g, chunk))
+                        at(first + 2 + chunk, lambda chunk=chunk: group_mean(g, chunk, on_vector=True))
+                        at(first + 3 + chunk, lambda chunk=chunk: quantise_mean(g, chunk))
 
         def plan_edges(st, slot):
             for chunk in range(CHUNKS):

import math
from contextlib import ExitStack

import concourse.mybir as mybir
from concourse.masks import make_identity

F32 = mybir.dt.float32
BF16 = mybir.dt.bfloat16
U32 = mybir.dt.uint32
U8 = mybir.dt.uint8
FP8X4 = mybir.dt.float8_e4m3fn_x4
ALU = mybir.AluOpType
ACT = mybir.ActivationFunctionType
AX = mybir.AxisListType

P = 128
PACK = 4
PAIR = 2
K_PASS = P * PACK
BANK = 512

N = 2048
F_IN = 512
F_OUT = 512
H = 8
SLOPE = 0.2
RISE = 1.0 - SLOPE
NO_EDGE = -1.0e9

ROW_TILES = N // P
CB = BANK // P
CHUNKS = ROW_TILES // CB
PASSES = N // K_PASS
JT = 2
PANEL = JT * P
PANELS = N // PANEL
LAG = 1
SPREAD = 3
VS = 4
JOIN = 20
TURN = 24
COL = 26
LEAD = 4
BASE = 0

FLOPS = 2 * N * F_IN * F_OUT + 2 * N * N * F_OUT


def tile_egatlayer_pa_kernel(
    tc,
    node_features,
    q,
    k,
    edges_features_distance,
    edges_features_bond,
    degree_matrix,
    Wv,
    w_bond,
    w_bond_contrib,
    w_gauss,
    out,
):
    nc = tc.nc
    bond_rows = edges_features_bond.rearrange("(p it) j -> p it j", it=ROW_TILES)
    dist_rows = edges_features_distance.rearrange("(p it) j -> p it j", it=ROW_TILES)
    degree_rows = degree_matrix.rearrange("(p it) j -> p it j", it=ROW_TILES)
    out_rows = out.rearrange("(p it) f -> p it f", it=ROW_TILES)
    nf_rows = node_features.rearrange("(g t p) c -> g p t c", t=PACK, p=P)
    wv_rows = Wv.rearrange("(u p e) f -> p u (e f)", u=PAIR, p=P, e=PAIR)

    with ExitStack() as ctx:
        const = ctx.enter_context(tc.tile_pool(name="const", bufs=1))
        keep = ctx.enter_context(tc.tile_pool(name="keep", bufs=1))
        edge = ctx.enter_context(tc.tile_pool(name="edge", bufs=2 * CHUNKS))
        stage = ctx.enter_context(tc.tile_pool(name="stage", bufs=2))
        small = ctx.enter_context(tc.tile_pool(name="small", bufs=4))
        work = ctx.enter_context(tc.tile_pool(name="work", bufs=2, reuse_waits="tile"))
        psum = ctx.enter_context(tc.psum_pool(name="psum", bufs=8))

        w_bond_sb = const.tile([P, 1], BF16)
        nc.sync.dma_start(out=w_bond_sb[:], in_=w_bond.partition_broadcast(P))
        w_contrib_sb = const.tile([P, 1], BF16)
        nc.sync.dma_start(out=w_contrib_sb[:], in_=w_bond_contrib.partition_broadcast(P))
        w_gauss_sb = const.tile([P, 1], BF16)
        nc.sync.dma_start(out=w_gauss_sb[:], in_=w_gauss.partition_broadcast(P))
        q_sb = const.tile([P, ROW_TILES * H], BF16)
        nc.sync.dma_start(out=q_sb[:], in_=q.rearrange("(p it) h -> p (it h)", it=ROW_TILES))
        k_sb = const.tile([P, ROW_TILES * H], BF16)
        nc.sync.dma_start(out=k_sb[:], in_=k.rearrange("(p it) h -> p (it h)", it=ROW_TILES))

        ident_f = const.tile([P, P], F32)
        make_identity(nc, ident_f[:])

        bond_weight = const.tile([P, 1], F32)
        nc.vector.tensor_tensor(out=bond_weight[:], in0=w_bond_sb[:], in1=w_contrib_sb[:], op=ALU.mult)
        gauss_weight = const.tile([P, 1], F32)
        nc.vector.tensor_copy(out=gauss_weight[:], in_=w_gauss_sb[:])

        q_plus_k = const.tile([P, ROW_TILES * H], F32)
        nc.vector.tensor_tensor(out=q_plus_k[:], in0=q_sb[:], in1=k_sb[:], op=ALU.add)
        by_head = q_plus_k[:].rearrange("p (it h) -> p it h", h=H)
        base_a = const.tile([P, ROW_TILES], F32)
        nc.vector.tensor_scalar_mul(out=base_a[:], in0=by_head[:, :, BASE], scalar1=1.0 / math.sqrt(H))
        d_raw = const.tile([P, ROW_TILES, H], F32)
        nc.vector.tensor_tensor(
            out=d_raw[:],
            in0=by_head,
            in1=by_head[:, :, BASE : BASE + 1].to_broadcast([P, ROW_TILES, H]),
            op=ALU.subtract,
        )
        d_flat = d_raw[:].rearrange("p it h -> p (it h)")
        a_sb = const.tile([P, ROW_TILES * H], F32)
        nc.vector.tensor_scalar_mul(out=a_sb[:], in0=d_flat, scalar1=1.0 / math.sqrt(H))
        neg_a = const.tile([P, ROW_TILES * H], F32)
        nc.vector.tensor_scalar_mul(out=neg_a[:], in0=d_flat, scalar1=-1.0 / math.sqrt(H))
        a_over_rise = const.tile([P, ROW_TILES * H], F32)
        nc.vector.tensor_scalar_mul(out=a_over_rise[:], in0=d_flat, scalar1=1.0 / (RISE * math.sqrt(H)))

        a_part = const.tile([P, ROW_TILES * H], F32)
        nc.vector.tensor_scalar_mul(out=a_part[:], in0=d_flat, scalar1=SLOPE / (RISE * math.sqrt(H)))

        a_t_ps = psum.tile([P, BANK], F32, tag="bank")
        nc.tensor.transpose(out=a_t_ps[:, :P], in_=a_sb[:], identity=ident_f[:])
        a_tile_top = const.tile([P, 1], F32)
        nc.vector.tensor_reduce(out=a_tile_top[:], in_=a_t_ps[:, :P], axis=AX.X, op=ALU.max)
        a_spread_ps = psum.tile([P, BANK], F32, tag="bank")
        nc.tensor.matmul(
            out=a_spread_ps[:, :P],
            lhsT=a_tile_top[:, 0:1].to_broadcast([P, P]),
            rhs=ident_f[:],
            start=True,
            stop=True,
        )
        a_top = const.tile([P, 1, H], F32)
        nc.vector.tensor_reduce(
            out=a_top[:, 0, :],
            in_=a_spread_ps[:, :P].rearrange("p (it h) -> p h it", h=H),
            axis=AX.X,
            op=ALU.max,
        )
        neg_a_top = const.tile([P, 1, H], F32)
        nc.vector.tensor_scalar_mul(out=neg_a_top[:, 0, :], in0=a_top[:, 0, :], scalar1=-1.0)

        v_codes = keep.tile([P, PASSES, F_OUT], U32, align_bytes=64)
        v_scales = keep.tile([P, PASSES, F_OUT], U8, align_bytes=64)

        attn_sum = keep.tile([P, PACK, N], F32)

        def new_panel(panel):
            return {
                "panel": panel,
                "top": stage.tile([P, PAIR * PANEL], F32, tag="panel_top", name="panel_top"),
                "e": [],
                "shared": [],
                "loads": [],
                "parts": [],
            }

        def load_edges(st, chunk):
            rows = slice(chunk * CB, (chunk + 1) * CB)
            cols = slice(st["panel"] * PANEL, (st["panel"] + 1) * PANEL)
            tiles = []
            for tag, rows_view in (("dist", dist_rows), ("bond", bond_rows), ("degree", degree_rows)):
                t = stage.tile([P, CB * PANEL], BF16, tag=tag, name="load_t")
                nc.sync.dma_start(out=t[:].rearrange("p (b j) -> p b j", b=CB), in_=rows_view[:, rows, cols])
                tiles.append(t)
            st["loads"].append(tiles)

        def scale_dist(st, chunk):
            e_t = edge.tile([P, CB * PANEL], F32, tag="e")
            for b in range(CB):
                it = chunk * CB + b
                nc.scalar.activation(
                    out=e_t[:, b * PANEL : (b + 1) * PANEL],
                    in_=st["loads"][chunk][0][:, b * PANEL : (b + 1) * PANEL],
                    func=ACT.Identity,
                    scale=gauss_weight[:, 0:1],
                    bias=base_a[:, it : it + 1],
                )
            st["e"].append(e_t)

        def make_mask(st, chunk):
            degree_t = st["loads"][chunk][2]
            nc.vector.tensor_scalar(
                out=degree_t[:], in0=degree_t[:], scalar1=0.0, scalar2=NO_EDGE / RISE, op0=ALU.is_le, op1=ALU.mult
            )

        def add_bond(st, chunk):
            e_t = st["e"][chunk]
            nc.vector.scalar_tensor_tensor(
                out=e_t[:], in0=st["loads"][chunk][1][:], scalar=bond_weight[:, 0:1], in1=e_t[:],
                op0=ALU.mult, op1=ALU.add,
            )

        def make_shared(st, chunk):
            shared_t = edge.tile([P, CB * PANEL], F32, tag="shared")
            nc.vector.scalar_tensor_tensor(
                out=shared_t[:], in0=st["e"][chunk][:], scalar=SLOPE / RISE, in1=st["loads"][chunk][2][:],
                op0=ALU.mult, op1=ALU.add,
            )
            st["shared"].append(shared_t)

        def raise_tops(st, chunk):
            shared_t = st["shared"][chunk]
            pairs = [shared_t[:, n * PAIR * PANEL : (n + 1) * PAIR * PANEL] for n in range(CB // PAIR)]
            if chunk > 0:
                pairs.append(st["top"][:])
            nc.vector.tensor_tensor(out=st["top"][:], in0=pairs[0], in1=pairs[-1], op=ALU.max)

        def raise_tops_again(st, chunk):
            shared_t = st["shared"][chunk]
            nc.vector.tensor_tensor(
                out=st["top"][:], in0=shared_t[:, PAIR * PANEL :], in1=st["top"][:], op=ALU.max
            )

        def join_tops(st):
            nc.vector.tensor_tensor(
                out=st["top"][:, :PANEL], in0=st["top"][:, :PANEL], in1=st["top"][:, PANEL:], op=ALU.max
            )

        def turn_tops(st):
            st["top_bank"] = psum.tile([P, BANK], F32, tag="bank", name="top_bank")
            for jt in range(JT):
                nc.tensor.transpose(
                    out=st["top_bank"][:, jt * P : (jt + 1) * P],
                    in_=st["top"][:, jt * P : (jt + 1) * P],
                    identity=ident_f[:],
                )

        def column_tops(st):
            st["e_top"] = small.tile([P, JT, 1], F32, tag="e_top", name="e_top")
            nc.vector.tensor_reduce(
                out=st["e_top"][:, :, 0],
                in_=st["top_bank"][:, : JT * P].rearrange("p (jt i) -> p jt i", jt=JT),
                axis=AX.X,
                op=ALU.max,
            )

        def negate_scores(st):
            st["neg_x"] = small.tile([P, JT, H], F32, tag="neg_x", name="neg_x")
            nc.vector.scalar_tensor_tensor(
                out=st["neg_x"][:],
                in0=st["e_top"][:].to_broadcast([P, JT, H]),
                scalar=-RISE / SLOPE,
                in1=neg_a_top[:].to_broadcast([P, JT, H]),
                op0=ALU.mult,
                op1=ALU.add,
            )

        def softmax_shifts(st):
            st["neg_shift"] = small.tile([P, JT, H], F32, tag="neg_shift", name="neg_shift")
            nc.vector.scalar_tensor_tensor(
                out=st["neg_shift"][:], in0=st["neg_x"][:], scalar=SLOPE, in1=st["neg_x"][:], op0=ALU.mult, op1=ALU.min
            )

        def load_wv(vwork):
            vs["wv_sb"] = vwork.tile([P, PACK, F_OUT], BF16, bufs=1, name="wv_sb")
            nc.sync.dma_start(out=vs["wv_sb"][:].rearrange("p (u e) f -> p u (e f)", u=PAIR), in_=wv_rows)

        def group_wv(vwork):
            vs["wv_grouped"] = vwork.tile([P, F_OUT, PACK], BF16, bufs=1, align_bytes=64, name="wv_grouped")
            nc.vector.tensor_copy(out=vs["wv_grouped"][:], in_=vs["wv_sb"][:].rearrange("p t f -> p f t"))

        def quantise_wv(vwork):
            vs["wv_codes"] = vwork.tile([P, F_OUT], U32, bufs=1, align_bytes=64, name="wv_codes")
            vs["wv_scales"] = vwork.tile([P, F_OUT], U8, bufs=1, align_bytes=64, name="wv_scales")
            nc.vector.quantize_mx(
                out=vs["wv_codes"][:].bitcast(FP8X4),
                scales=vs["wv_scales"][:],
                in_=vs["wv_grouped"][:].rearrange("p f t -> p (f t)"),
            )

        def load_nodes(vwork, g):
            vs["nf", g] = vwork.tile([P, PACK, F_IN], BF16, tag="nf_sb", align_bytes=64, name="nf_sb")
            nc.sync.dma_start(out=vs["nf", g][:], in_=nf_rows[g])

        def turn_nodes(vwork, g):
            nf_grouped = vwork.tile([P, PACK, P, PACK], BF16, bufs=1, align_bytes=64)
            for half in range(PAIR):
                words_ps = psum.tile([P, PAIR, PAIR, P], F32, tag="bank", name="words_ps")
                for s in range(PAIR):
                    words = vs["nf", g][:, PAIR * half + s, :].bitcast(F32)
                    for u in range(PAIR):
                        nc.tensor.transpose(
                            out=words_ps[:, s, u, :], in_=words[:, u * P : (u + 1) * P], identity=ident_f[:]
                        )
                nc.scalar.copy(
                    out=nf_grouped[:, PAIR * half : PAIR * (half + 1), :, :]
                    .rearrange("p t r k -> p (t r k)")
                    .bitcast(F32)
                    .rearrange("p (t r u) -> p t r u", t=PAIR, u=PAIR),
                    in_=words_ps[:].rearrange("p t u r -> p t r u"),
                )
            vs["nf_grouped", g] = nf_grouped

        def quantise_nodes(vwork, g):
            nf_codes = vwork.tile([P, PACK * P], U32, bufs=1, align_bytes=64)
            nf_scales = vwork.tile([P, PACK * P], U8, bufs=1, align_bytes=64)
            nc.vector.quantize_mx(
                out=nf_codes[:].bitcast(FP8X4),
                scales=nf_scales[:],
                in_=vs["nf_grouped", g][:].rearrange("p t r s -> p (t r s)"),
            )
            vs["nf_codes", g] = (nf_codes, nf_scales)

        def multiply_nodes(vwork, g):
            nf_codes, nf_scales = vs["nf_codes", g]
            v_planes = vwork.tile([P, PACK, F_OUT], BF16, bufs=1)
            for t in range(PACK):
                v_ps = psum.tile([P, F_OUT], F32, tag="bank")
                nc.tensor.matmul_mx(
                    out=v_ps[:],
                    lhsT=nf_codes[:, t * P : (t + 1) * P].bitcast(FP8X4),
                    lhsT_scale=nf_scales[:, t * P : (t + 1) * P],
                    rhs=vs["wv_codes"][:].bitcast(FP8X4),
                    rhs_scale=vs["wv_scales"][:],
                    start=True,
                    stop=True,
                )
                nc.scalar.activation(
                    out=v_planes[:, t, :], in_=v_ps[:], func=ACT.Copy, scale=1.0 / math.sqrt(F_IN)
                )
            vs["v_planes", g] = v_planes

        def group_v(vwork, g):
            vs["v_grouped", g] = vwork.tile([P, F_OUT, PACK], BF16, bufs=1, align_bytes=64, name="v_grouped")
            nc.vector.tensor_copy(out=vs["v_grouped", g][:], in_=vs["v_planes", g][:].rearrange("p t f -> p f t"))

        def quantise_v(vwork, g):
            nc.vector.quantize_mx(
                out=v_codes[:, g, :].bitcast(FP8X4),
                scales=v_scales[:, g, :],
                in_=vs["v_grouped", g][:].rearrange("p f t -> p (f t)"),
            )

        def plan_v(vwork):
            at(1, lambda: group_wv(vwork))
            at(3, lambda: quantise_wv(vwork))
            for g in range(PASSES):
                first = 4 * g
                at(first + 1, lambda g=g: turn_nodes(vwork, g))
                at(first + 4, lambda g=g: quantise_nodes(vwork, g))
                at(first + 5, lambda g=g: multiply_nodes(vwork, g))
                at(first + 8, lambda g=g: group_v(vwork, g))
                at(first + 9, lambda g=g: quantise_v(vwork, g))
                if g + 2 < PASSES:
                    at(first + 3, lambda g=g: load_nodes(vwork, g + 2))

        vs = {}

        def new_head():
            return {
                "w": [work.tile([P, N], F32, tag="w", bufs=6, name="w") for jt in range(JT)],
                "sums": small.tile([P, JT, CHUNKS], F32, tag="sums", name="sums"),
            }

        def scalar_tiles(panel, h, chunk):
            if h == BASE:
                return ()
            if panel == PANELS - 1:
                return (3,)
            return (1, 2, 3) if chunk == 0 else (2, 3)

        def make_part(st, h, chunk):
            e_t = st["e"][chunk]
            head_t = work.tile([P, CB * PANEL], F32, tag="head", bufs=7, align_bytes=64, name="head_t")
            if h == BASE and st["panel"] == 0:
                nc.scalar.activation(out=head_t[:], in_=e_t[:], func=ACT.Relu)
            elif h == BASE:
                nc.vector.tensor_scalar_max(out=head_t[:], in0=e_t[:], scalar1=0.0)
            else:
                for b in range(CB):
                    col = (chunk * CB + b) * H + h
                    cols = slice(b * PANEL, (b + 1) * PANEL)
                    if b in scalar_tiles(st["panel"], h, chunk):
                        nc.scalar.activation(
                            out=head_t[:, cols], in_=e_t[:, cols], func=ACT.Relu, bias=a_sb[:, col : col + 1]
                        )
                    else:
                        nc.vector.tensor_scalar(
                            out=head_t[:, cols],
                            in0=e_t[:, cols],
                            scalar1=neg_a[:, col : col + 1],
                            scalar2=a_over_rise[:, col : col + 1],
                            op0=ALU.max,
                            op1=ALU.add,
                        )
            st["parts"].append(head_t)

        def exponentials(st, head, h, chunk):
            shared_t = st["shared"][chunk]
            head_t = st["parts"][h * CHUNKS + chunk]
            for jt in range(JT):
                bank = psum.tile([P, BANK], F32, tag="bank")
                for b in range(CB):
                    cols = slice(b * PANEL + jt * P, b * PANEL + (jt + 1) * P)
                    nc.tensor.matmul(
                        out=bank[:, b * P : (b + 1) * P], lhsT=shared_t[:, cols], rhs=ident_f[:],
                        is_transpose=True, start=True, stop=False,
                    )
                    nc.tensor.matmul(
                        out=bank[:, b * P : (b + 1) * P], lhsT=head_t[:, cols], rhs=ident_f[:],
                        is_transpose=True, start=False, stop=b not in scalar_tiles(st["panel"], h, chunk),
                    )
                    if b in scalar_tiles(st["panel"], h, chunk):
                        col = (chunk * CB + b) * H + h
                        nc.tensor.matmul(
                            out=bank[:, b * P : (b + 1) * P], lhsT=a_part[:, col : col + 1].to_broadcast([P, P]),
                            rhs=ident_f[:], is_transpose=True, start=False, stop=True,
                        )
                nc.scalar.activation(
                    out=head["w"][jt][:, chunk * BANK : (chunk + 1) * BANK],
                    in_=bank[:],
                    func=ACT.Exp,
                    bias=st["neg_shift"][:, jt, h : h + 1],
                    scale=RISE,
                    accum_out=head["sums"][:, jt, chunk : chunk + 1],
                )

        def add_sums(head):
            head["total"] = small.tile([P, JT], F32, tag="total", name="total")
            nc.vector.tensor_reduce(out=head["total"][:], in_=head["sums"][:], axis=AX.X, op=ALU.add)

        def invert_sums(head):
            head["inverse"] = small.tile([P, JT], F32, tag="inverse", name="inverse")
            nc.vector.reciprocal(out=head["inverse"][:], in_=head["total"][:])

        def add_head(panel, head, h, jt, cols):
            plane = attn_sum[:, (panel % PAIR) * JT + jt, cols]
            scale = head["inverse"][:, jt : jt + 1]
            if h == 0:
                nc.vector.tensor_scalar_mul(out=plane, in0=head["w"][jt][:, cols], scalar1=scale)
            else:
                nc.vector.scalar_tensor_tensor(
                    out=plane, in0=head["w"][jt][:, cols], scalar=scale, in1=plane, op0=ALU.mult, op1=ALU.add
                )

        def group_mean(g, chunk, on_vector=False):
            cols = slice(chunk * BANK, (chunk + 1) * BANK)
            grouped = work.tile([P, BANK, PACK], BF16, tag="head", bufs=7, align_bytes=64, name="grouped")
            planes = attn_sum[:, :, cols].rearrange("p t i -> p i t")
            if on_vector:
                nc.vector.tensor_scalar_mul(out=grouped[:], in0=planes, scalar1=1.0 / H)
            else:
                nc.scalar.activation(out=grouped[:], in_=planes, func=ACT.Copy, scale=1.0 / H)
            state["grouped", g, chunk] = grouped

        def quantise_mean(g, chunk):
            cols = slice(chunk * BANK, (chunk + 1) * BANK)
            nc.vector.quantize_mx(
                out=attn_codes[:, g, cols].bitcast(FP8X4),
                scales=attn_scales[PACK * g :, cols],
                in_=state["grouped", g, chunk][:].rearrange("p i t -> p (i t)"),
            )

        state = {"slot": 0}
        schedule = {}

        def at(slot, task):
            schedule.setdefault(slot, []).append(task)

        def run_slot():
            for task in schedule.get(state["slot"], []):
                task()
            state["slot"] = state["slot"] + 1

        def plan_head(panel, head, h, slot):
            if panel == PANELS - 1 and h == H - 1:
                return
            at(slot + LAG, lambda: add_sums(head))
            at(slot + LAG + 1, lambda: invert_sums(head))
            last = h == H - 1 and panel % PAIR == PAIR - 1
            g = panel // PAIR
            first = slot + LAG + 2
            for half in range(2):
                for jt in range(JT):
                    cols = slice(half * N // 2, (half + 1) * N // 2)
                    at(min(first + 2 * half + jt, PANELS * H * CHUNKS - 1), lambda jt=jt, cols=cols: add_head(panel, head, h, jt, cols))
                if last:
                    for chunk in (2 * half, 2 * half + 1):
                        at(first + 2 + chunk, lambda chunk=chunk: group_mean(g, chunk, on_vector=True))
                        at(first + 3 + chunk, lambda chunk=chunk: quantise_mean(g, chunk))

        def plan_edges(st, slot):
            for chunk in range(CHUNKS):
                first = slot + SPREAD * chunk
                at(first + 0, lambda chunk=chunk: load_edges(st, chunk))
                at(first + 1, lambda chunk=chunk: scale_dist(st, chunk))
                at(first + VS, lambda chunk=chunk: make_mask(st, chunk))
                at(first + VS + 1, lambda chunk=chunk: add_bond(st, chunk))
                at(first + VS + 2, lambda chunk=chunk: make_shared(st, chunk))
                at(first + VS + 3, lambda chunk=chunk: raise_tops(st, chunk))
                if chunk > 0:
                    at(first + VS + 4, lambda chunk=chunk: raise_tops_again(st, chunk))
            at(slot + JOIN, lambda: join_tops(st))
            at(slot + TURN, lambda: turn_tops(st))
            at(slot + COL, lambda: column_tops(st))
            at(slot + COL + 1, lambda: negate_scores(st))
            at(slot + COL + 1, lambda: softmax_shifts(st))

        def run_head(st, h):
            if h == 0 and st["panel"] + 1 < PANELS:
                state["next"] = new_panel(st["panel"] + 1)
                plan_edges(state["next"], state["slot"])
            head = new_head()
            for chunk in range(CHUNKS):
                ahead = h * CHUNKS + chunk + LEAD
                if ahead < H * CHUNKS:
                    make_part(st, ahead // CHUNKS, ahead % CHUNKS)
                elif "next" in state and state["next"]["panel"] > st["panel"]:
                    make_part(state["next"], 0, ahead - H * CHUNKS)
                exponentials(st, head, h, chunk)
                run_slot()
            plan_head(st["panel"], head, h, state["slot"])
            return head

        st = new_panel(0)
        with tc.manual_schedule(engines={mybir.EngineType.DVE, mybir.EngineType.Activation, mybir.EngineType.PE}):
            for chunk in range(CHUNKS):
                load_edges(st, chunk)
                scale_dist(st, chunk)
                add_bond(st, chunk)
                make_mask(st, chunk)
                if chunk > 0:
                    raise_tops(st, chunk - 1)
                make_shared(st, chunk)
                if chunk > 1:
                    raise_tops_again(st, chunk - 1)
            for chunk in range(LEAD):
                make_part(st, 0, chunk)
            raise_tops(st, CHUNKS - 1)
            raise_tops_again(st, CHUNKS - 1)
            join_tops(st)
            turn_tops(st)
            column_tops(st)
            negate_scores(st)
            softmax_shifts(st)

        with tc.manual_schedule(engines={mybir.EngineType.DVE, mybir.EngineType.Activation, mybir.EngineType.PE}):
            with tc.tile_pool(name="vwork", bufs=2) as vwork:
                load_wv(vwork)
                load_nodes(vwork, 0)
                load_nodes(vwork, 1)
                plan_v(vwork)
                for h in range(6):
                    run_head(st, h)

            late = ctx.enter_context(tc.tile_pool(name="late", bufs=2, reuse_waits="tile"))
            attn_codes = late.tile([P, PASSES, N], U32, bufs=1, align_bytes=64)
            attn_scales = late.tile([P, N], U8, bufs=1, align_bytes=64)
            for h in range(6, H):
                run_head(st, h)
            for panel in range(1, PANELS):
                st = state["next"]
                for h in range(H):
                    head = run_head(st, h)
        def out_pass(out_ps, it, g):
            rows = slice(it * P, (it + 1) * P)
            nc.tensor.matmul_mx(
                out=out_ps[:],
                lhsT=attn_codes[:, g, rows].bitcast(FP8X4),
                lhsT_scale=attn_scales[PACK * g :, rows],
                rhs=v_codes[:, g, :].bitcast(FP8X4),
                rhs_scale=v_scales[:, g, :],
                start=(g == 0),
                stop=(g == PASSES - 1),
            )

        def finish_rows(out_ps, it):
            elu_t = work.tile([P, 2, F_OUT], F32, tag="w", bufs=6, name="elu_t")
            nc.scalar.activation(out=elu_t[:, 0, :], in_=out_ps[:], func=ACT.Exp)
            if it % 4 != 3:
                nc.scalar.activation(out=elu_t[:, 1, :], in_=out_ps[:], func=ACT.Relu)
                nc.vector.tensor_scalar(
                    out=elu_t[:, 0, :], in0=elu_t[:, 0, :], scalar1=1.0, scalar2=-1.0, op0=ALU.min, op1=ALU.add
                )
                nc.vector.tensor_tensor(out=elu_t[:, 0, :], in0=elu_t[:, 0, :], in1=elu_t[:, 1, :], op=ALU.add)
            else:
                nc.vector.tensor_scalar(
                    out=elu_t[:, 1, :], in0=out_ps[:], scalar1=0.0, scalar2=-1.0, op0=ALU.max, op1=ALU.add
                )
                nc.vector.scalar_tensor_tensor(
                    out=elu_t[:, 0, :], in0=elu_t[:, 0, :], scalar=1.0, in1=elu_t[:, 1, :], op0=ALU.min, op1=ALU.add
                )
            nc.sync.dma_start(out=out_rows[:, it, :], in_=elu_t[:, 0, :])

        with tc.manual_schedule(engines={mybir.EngineType.DVE, mybir.EngineType.Activation, mybir.EngineType.PE}):
            add_sums(head)
            invert_sums(head)
            for chunk in range(CHUNKS):
                for jt in range(JT):
                    add_head(PANELS - 1, head, H - 1, jt, slice(chunk * BANK, (chunk + 1) * BANK))
            banks = []
            for it in range(8):
                banks.append(psum.tile([P, F_OUT], F32, tag="bank", name="out_ps"))
                for g in range(PASSES - 1):
                    out_pass(banks[it], it, g)
            for chunk in range(2):
                group_mean(PASSES - 1, chunk)
            quantise_mean(PASSES - 1, 0)
            for chunk in range(2, CHUNKS):
                group_mean(PASSES - 1, chunk, on_vector=True)
            for chunk in range(1, CHUNKS):
                quantise_mean(PASSES - 1, chunk)
            for it in range(ROW_TILES):
                if it >= 8:
                    banks.append(psum.tile([P, F_OUT], F32, tag="bank", name="out_ps"))
                    for g in range(PASSES - 1):
                        out_pass(banks[it], it, g)
                out_pass(banks[it], it, PASSES - 1)
                finish_rows(banks[it], it)
